import numpy as np
import ml_dtypes


def mxq(x, axis, fmt="e4m3"):
    dtype, down = {"e4m3": (ml_dtypes.float8_e4m3fn, 7), "e5m2": (ml_dtypes.float8_e5m2, 14)}[fmt]
    v = np.moveaxis(np.asarray(x, np.float32).astype(ml_dtypes.bfloat16).astype(np.float64), axis, -1)
    blocks = v.reshape(v.shape[:-1] + (-1, 32))
    amax = np.abs(blocks).max(-1, keepdims=True)
    byte = np.maximum(np.where(amax > 0, np.frexp(amax)[1] - 1 + 127, 0) - down, 1)
    scale = np.exp2(byte - 127.0)
    codes = (blocks / scale).astype(np.float32).astype(dtype).astype(np.float64)
    return np.moveaxis((codes * scale).reshape(v.shape), -1, axis)


WIDE = False


def mx_kscale(k):
    if not WIDE:
        return np.ones(k)
    levels = np.array([10, -10, 5, -5, 0])
    if k % 512:
        return np.exp2(np.random.permutation(np.resize(levels, k // 32))).repeat(32)
    a = np.empty((k // 512, 16))
    for p in range(k // 512):
        a[p, :8] = np.random.permutation(np.resize(levels, 8))
        for g in range(8):
            far = levels[np.abs(levels - a[p, g]) >= 10]
            a[p, g + 8] = far[np.random.randint(len(far))]
    return np.exp2(a.ravel()).repeat(32)


BF16 = ml_dtypes.bfloat16


def bf(x):
    return np.asarray(x, np.float32).astype(BF16)


def f64(x):
    return np.asarray(x).astype(np.float64)


B, T, D, K, CD, CF, M = 8, 16, 1024, 32, 128, 512, 256
LN_EPS = 1e-5


def setup_inputs():
    s = mx_kscale(D)
    t = mx_kscale(CF)
    return {
        "h": bf(np.random.standard_normal((B, T, D)) * s),
        "mu_w1_h": bf(np.random.standard_normal((D, CF)) / np.sqrt(D) / s[:, None]),
        "code_mu": bf(np.random.standard_normal((K, CF)) * 0.4),
        "mu_b1": bf(np.random.standard_normal(CF) * 0.2),
        "ln_g": bf((1.0 + 0.1 * np.random.standard_normal(CF)) * t),
        "ln_b": bf(np.random.standard_normal(CF) * 0.2 * t),
        "mu_w2": bf(np.random.standard_normal((CF, CF)) / np.sqrt(CF) / t[:, None]),
        "mu_b2": bf(np.random.standard_normal(CF) * 0.2),
    }


def reference(h, mu_w1_h, code_mu, mu_b1, ln_g, ln_b, mu_w2, mu_b2):
    hp = mxq(f64(h), 2, "e4m3") @ mxq(f64(mu_w1_h), 0, "e4m3")
    mu_pre = hp[:, :, None, :] + f64(code_mu) + f64(mu_b1)
    mean = mu_pre.mean(-1, keepdims=True)
    var = np.square(mu_pre - mean).mean(-1, keepdims=True)
    mu_ln = (mu_pre - mean) * (1.0 / np.sqrt(var + LN_EPS)) * f64(ln_g) + f64(ln_b)
    return np.tanh((mxq(mu_ln, 3, "e4m3") @ mxq(f64(mu_w2), 0, "e4m3")) + f64(mu_b2))

@@ -1,0 +1,395 @@
+from contextlib import ExitStack
+
+from concourse import mybir
+from concourse.masks import make_identity
+
+F32 = mybir.dt.float32
+BF16 = mybir.dt.bfloat16
+U32 = mybir.dt.uint32
+U8 = mybir.dt.uint8
+FP8X4 = mybir.dt.float8_e4m3fn_x4
+ALU = mybir.AluOpType
+ACT = mybir.ActivationFunctionType
+AX = mybir.AxisListType
+
+P = 128
+TOK = 128
+D_IN = 1024
+CF = 512
+NCODE = 32
+LN_EPS = 1e-5
+CG = 4
+ROUNDS = NCODE // CG
+W = CG * TOK
+LEAD = 2
+
+FLOPS = 2 * TOK * D_IN * CF + 2 * TOK * NCODE * CF * CF
+
+ROW_B1 = 32
+ROW_G = 40
+ROW_B = 48
+ROW_B2 = 56
+W1_V = 352
+
+
+def regroup(eng_copy, dst, src):
+    eng_copy(
+        out=dst.rearrange("p (c i) t -> p c t i", i=4),
+        in_=src.rearrange("p t (c i) -> p c t i", i=4),
+    )
+
+
+def regroup_w1(eng_copy, dst, src, m0, m1):
+    eng_copy(
+        out=dst.rearrange("p (t m) j -> p t m j", t=4)[:, :, m0:m1],
+        in_=src.rearrange("p j (m t) -> p t m j", t=4)[:, :, m0:m1],
+    )
+
+
+def tile_mixtureconfounderprior_pa_kernel(
+    tc, h, mu_w1_h, code_mu, mu_b1, ln_g, ln_b, mu_w2, mu_b2, out
+):
+    nc = tc.nc
+    h2 = h.rearrange("b t d -> (b t) d")
+    out3 = out.rearrange("b t k n -> (b t) k n")
+
+    with ExitStack() as ctx:
+        keep = ctx.enter_context(tc.tile_pool(name="keep", bufs=1))
+        work = ctx.enter_context(tc.tile_pool(name="work", bufs=3))
+        psr = ctx.enter_context(tc.psum_pool(name="psr", bufs=2))
+        pso = ctx.enter_context(tc.psum_pool(name="pso", bufs=6))
+        ctx.enter_context(tc.manual_schedule())
+
+        h_sb = keep.tile([P, D_IN], BF16)
+        nc.sync.dma_start(out=h_sb[:], in_=h2)
+        w1_raw = keep.tile([P, 2, 4, CF], BF16)
+        for g in range(2):
+            nc.sync.dma_start(
+                out=w1_raw[:, g],
+                in_=mu_w1_h[512 * g : 512 * (g + 1), :].rearrange("(p j) c -> p j c", j=4),
+            )
+        w2_raw = keep.tile([P, 4, CF], BF16)
+        nc.sync.dma_start(out=w2_raw[:], in_=mu_w2.rearrange("(p t) n -> p t n", t=4))
+        sm_raw = keep.tile([P, CF], BF16)
+        nc.scalar.dma_start(out=sm_raw[0:NCODE, :], in_=code_mu)
+        nc.scalar.dma_start(out=sm_raw[ROW_B1 : ROW_B1 + 8, :], in_=mu_b1.partition_broadcast(8))
+        nc.scalar.dma_start(out=sm_raw[ROW_G : ROW_G + 8, :], in_=ln_g.partition_broadcast(8))
+        nc.scalar.dma_start(out=sm_raw[ROW_B : ROW_B + 8, :], in_=ln_b.partition_broadcast(8))
+        nc.scalar.dma_start(out=sm_raw[ROW_B2 : ROW_B2 + 8, :], in_=mu_b2.partition_broadcast(8))
+        nc.vector.memset(sm_raw[64:128, :].bitcast(F32), 0.0)
+
+        ident = keep.tile([P, P], F32)
+        make_identity(nc, ident[:])
+        ident_bf = keep.tile([P, P], BF16)
+        make_identity(nc, ident_bf[:])
+        ones = keep.tile([P, P], F32)
+        nc.vector.memset(ones[:], 1.0 / CF)
+        eps = keep.tile([P, 1], F32)
+        nc.vector.memset(eps[:], LN_EPS)
+        warm = keep.tile([P, 1], F32)
+        nc.scalar.activation(out=warm[:], in_=eps[:], func=ACT.Sqrt)
+
+        h_w = h_sb[:].bitcast(F32)
+        xt = pso.tile([P, 2, 2, P], F32, tag="o")
+        for g in range(2):
+            for u in range(2):
+                nc.tensor.transpose(
+                    xt[:, g, u, :], h_w[:, 256 * g + u : 256 * (g + 1) : 2], ident[:]
+                )
+        hg = keep.tile([P, 2, TOK, 4], BF16, align_bytes=64)
+        nc.vector.tensor_copy(
+            out=hg[:].bitcast(F32), in_=xt[:].rearrange("p g u r -> p g r u")
+        )
+        smT_ps = pso.tile([P, 4, P], BF16, tag="o")
+        for t in range(4):
+            nc.tensor.transpose(smT_ps[:, t, :], sm_raw[:, t : CF : 4], ident_bf[:])
+        smT = keep.tile([P, 4, 64], F32)
+        nc.scalar.copy(out=smT[:], in_=smT_ps[:, :, 0:64])
+
+        w1g = keep.tile([P, 2, CF, 4], BF16, align_bytes=64)
+        w1_codes = keep.tile([P, 2, CF], U32, align_bytes=64)
+        w1_scales = keep.tile([P, 2, CF], U8, align_bytes=64)
+        h_codes = keep.tile([P, 2 * TOK], U32, align_bytes=64)
+        h_scales = keep.tile([P, 2 * TOK], U8, align_bytes=64)
+
+        regroup_w1(nc.vector.tensor_copy, w1g[:, 0], w1_raw[:, 0], 0, W1_V // 4)
+        regroup_w1(nc.scalar.copy, w1g[:, 0], w1_raw[:, 0], W1_V // 4, P)
+        nc.vector.quantize_mx(
+            out=h_codes[:].bitcast(FP8X4),
+            scales=h_scales[:],
+            in_=hg[:].rearrange("p g r t -> p (g r t)"),
+        )
+        cm1 = keep.tile([P, 4, NCODE], F32)
+        nc.vector.tensor_tensor(
+            out=cm1[:],
+            in0=smT[:, :, 0:NCODE],
+            in1=smT[:, :, ROW_B1 : ROW_B1 + 1].to_broadcast([P, 4, NCODE]),
+            op=ALU.add,
+        )
+        cms = keep.tile([P, NCODE], F32)
+        nc.vector.tensor_reduce(
+            out=cms[:], in_=cm1[:].rearrange("p t c -> p c t"), axis=AX.X, op=ALU.add
+        )
+        mc_ps = pso.tile([P, NCODE], F32, tag="o")
+        nc.tensor.matmul(mc_ps[:], lhsT=ones[:], rhs=cms[:], start=True, stop=True)
+        nc.vector.quantize_mx(
+            out=w1_codes[:, 0, :].bitcast(FP8X4),
+            scales=w1_scales[:, 0, :],
+            in_=w1g[:, 0].rearrange("p c t -> p (c t)"),
+        )
+        regroup_w1(nc.vector.tensor_copy, w1g[:, 1], w1_raw[:, 1], 0, W1_V // 4)
+        regroup_w1(nc.scalar.copy, w1g[:, 1], w1_raw[:, 1], W1_V // 4, P)
+        nc.vector.quantize_mx(
+            out=w1_codes[:, 1, :].bitcast(FP8X4),
+            scales=w1_scales[:, 1, :],
+            in_=w1g[:, 1].rearrange("p c t -> p (c t)"),
+        )
+
+        hpT_ps = [pso.tile([P, TOK], F32, tag="o", name="hpT_ps%d" % t) for t in range(4)]
+        hp_ps = pso.tile([P, CF], F32, tag="o")
+        for g in range(2):
+            for t in range(4):
+                nc.tensor.matmul_mx(
+                    out=hpT_ps[t][:],
+                    lhsT=w1_codes[:, g, P * t : P * (t + 1)].bitcast(FP8X4),
+                    lhsT_scale=w1_scales[:, g, P * t : P * (t + 1)],
+                    rhs=h_codes[:, TOK * g : TOK * (g + 1)].bitcast(FP8X4),
+                    rhs_scale=h_scales[:, TOK * g : TOK * (g + 1)],
+                    start=(g == 0),
+                    stop=(g == 1),
+                )
+            nc.tensor.matmul_mx(
+                out=hp_ps[:],
+                lhsT=h_codes[:, TOK * g : TOK * (g + 1)].bitcast(FP8X4),
+                lhsT_scale=h_scales[:, TOK * g : TOK * (g + 1)],
+                rhs=w1_codes[:, g, :].bitcast(FP8X4),
+                rhs_scale=w1_scales[:, g, :],
+                start=(g == 0),
+                stop=(g == 1),
+            )
+        c_sb = keep.tile([P, 4, NCODE], F32)
+        nc.vector.tensor_tensor(
+            out=c_sb[:],
+            in0=cm1[:],
+            in1=mc_ps[:].unsqueeze(1).to_broadcast([P, 4, NCODE]),
+            op=ALU.subtract,
+        )
+        c2 = keep.tile([P, 4, NCODE], F32)
+        nc.vector.tensor_scalar_mul(out=c2[:], in0=c_sb[:], scalar1=2.0 / CF)
+        csq = keep.tile([P, 4, NCODE], F32)
+        nc.vector.tensor_tensor(out=csq[:], in0=c_sb[:], in1=c_sb[:], op=ALU.mult)
+        cvs = keep.tile([P, NCODE], F32)
+        nc.vector.tensor_reduce(
+            out=cvs[:], in_=csq[:].rearrange("p t c -> p c t"), axis=AX.X, op=ALU.add
+        )
+        w2g = keep.tile([P, CF, 4], BF16, align_bytes=64)
+        regroup(nc.scalar.copy, w2g[:, 0 : CF // 2], w2_raw[:, :, 0 : CF // 2])
+        hpT_v = keep.tile([P, 2, TOK], F32)
+        hpT_s = keep.tile([P, 2, TOK], F32)
+        for i in range(2):
+            nc.vector.tensor_copy(out=hpT_v[:, i, :], in_=hpT_ps[i][:])
+            nc.scalar.copy(out=hpT_s[:, i, :], in_=hpT_ps[2 + i][:])
+        hpT = [hpT_v[:, 0, :], hpT_v[:, 1, :], hpT_s[:, 0, :], hpT_s[:, 1, :]]
+        regroup(nc.scalar.copy, w2g[:, CF // 2 : CF], w2_raw[:, :, CF // 2 : CF])
+        v_ps = pso.tile([P, NCODE], F32, tag="o")
+        nc.tensor.matmul(v_ps[:], lhsT=ones[:], rhs=cvs[:], start=True, stop=False)
+        for t in range(4):
+            nc.tensor.matmul(v_ps[:], lhsT=hpT[t], rhs=c2[:, t, :], start=False, stop=(t == 3))
+
+        st = keep.tile([P, 6], F32)
+        nc.vector.bn_stats(out=st[:], in_=hp_ps[:])
+        mv = keep.tile([P, 2], F32)
+        nc.vector.bn_aggr(out=mv[:], in_=st[:])
+        vhe = keep.tile([P, 1], F32)
+        nc.vector.tensor_scalar_add(out=vhe[:], in0=mv[:, 1:2], scalar1=LN_EPS)
+        mh_ps = pso.tile([P, TOK], F32, tag="o")
+        nc.tensor.transpose(mh_ps[:], mv[:, 0:1].to_broadcast([P, P]), ident[:])
+        std = keep.tile([P, NCODE], F32)
+        nc.scalar.activation(out=std[:], in_=v_ps[:], func=ACT.Sqrt, bias=vhe[:, 0:1])
+        nc.scalar.activation(out=warm[:], in_=eps[:], func=ACT.Tanh)
+        w2_codes = keep.tile([P, CF], U32, align_bytes=64)
+        w2_scales = keep.tile([P, CF], U8, align_bytes=64)
+        nc.vector.quantize_mx(
+            out=w2_codes[:].bitcast(FP8X4),
+            scales=w2_scales[:],
+            in_=w2g[:].rearrange("p c t -> p (c t)"),
+        )
+        r_sb = keep.tile([P, NCODE], F32)
+        nc.vector.reciprocal(out=r_sb[:], in_=std[:])
+        a_sb = keep.tile([P, 4, TOK], F32)
+        nc.vector.tensor_tensor(
+            out=a_sb[:, 0:2, :],
+            in0=hpT_v[:],
+            in1=mh_ps[:].unsqueeze(1).to_broadcast([P, 2, TOK]),
+            op=ALU.subtract,
+        )
+        nc.vector.tensor_tensor(
+            out=a_sb[:, 2:4, :],
+            in0=hpT_s[:],
+            in1=mh_ps[:].unsqueeze(1).to_broadcast([P, 2, TOK]),
+            op=ALU.subtract,
+        )
+        b2_bc = keep.tile([P, CF], F32)
+
+        tiles = {}
+
+        def bcast_r(rd):
+            for cl in range(CG):
+                code = CG * rd + cl
+                if rd == 0:
+                    r_one = pso.tile([P, TOK], F32, tag="o", name="r_one")
+                    tiles[("r", rd, cl)] = r_one[:]
+                else:
+                    if cl == 0:
+                        r_ps = psr.tile([P, CG, TOK], F32, tag="r", name="r_ps")
+                        tiles[("rt", rd)] = r_ps
+                    tiles[("r", rd, cl)] = tiles[("rt", rd)][:, cl, :]
+                nc.tensor.transpose(
+                    tiles[("r", rd, cl)], r_sb[:, code : code + 1].to_broadcast([P, P]), ident[:]
+                )
+
+        def load_b2():
+            b2_ps = pso.tile([P, CF], F32, tag="o", name="b2_ps")
+            nc.tensor.matmul(
+                b2_ps[:],
+                lhsT=ident_bf[:, ROW_B2 : ROW_B2 + 1].to_broadcast([P, P]),
+                rhs=sm_raw[:],
+                start=True,
+                stop=True,
+            )
+            nc.scalar.copy(out=b2_bc[:], in_=b2_ps[:])
+
+        def normalise(rd, cls):
+            if cls[0] == 0:
+                z_new = work.tile([P, 4, CG, TOK], F32, name="z")
+                tiles[("z", rd)] = z_new
+            z = tiles[("z", rd)]
+            for cl in cls:
+                code = CG * rd + cl
+                for t in range(4):
+                    nc.vector.scalar_tensor_tensor(
+                        out=z[:, t, cl, :],
+                        in0=a_sb[:, t, :],
+                        scalar=c_sb[:, t, code : code + 1],
+                        in1=tiles[("r", rd, cl)],
+                        op0=ALU.add,
+                        op1=ALU.mult,
+                    )
+
+        def gain_bias(rd, planes, eng):
+            z = tiles[("z", rd)]
+            if ("m", rd) not in tiles:
+                m_new = work.tile([P, 4, W], BF16, name="m")
+                tiles[("m", rd)] = m_new
+            m = tiles[("m", rd)]
+            for t in planes:
+                if eng == "s":
+                    nc.scalar.activation(
+                        out=m[:, t, :],
+                        in_=z[:, t].rearrange("p c r -> p (c r)"),
+                        func=ACT.Identity,
+                        scale=smT[:, t, ROW_G : ROW_G + 1],
+                        bias=smT[:, t, ROW_B : ROW_B + 1],
+                    )
+                else:
+                    engine = nc.gpsimd if eng == "g" else nc.vector
+                    engine.tensor_scalar(
+                        out=m[:, t, :],
+                        in0=z[:, t].rearrange("p c r -> p (c r)"),
+                        scalar1=smT[:, t, ROW_G : ROW_G + 1],
+                        scalar2=smT[:, t, ROW_B : ROW_B + 1],
+                        op0=ALU.mult,
+                        op1=ALU.add,
+                    )
+
+        def regroup_mu(rd, rv):
+            m = tiles[("m", rd)]
+            mg = work.tile([P, W, 4], BF16, align_bytes=64, name="mg")
+            tiles[("mg", rd)] = mg
+            if rv > 0:
+                regroup(nc.vector.tensor_copy, mg[:, 0:rv], m[:, :, 0:rv])
+            if rv < W:
+                regroup(nc.scalar.copy, mg[:, rv:W], m[:, :, rv:W])
+
+        def quantise_mu(rd):
+            mg = tiles[("mg", rd)]
+            mu_codes = work.tile([P, W], U32, align_bytes=64, name="mu_codes")
+            mu_scales = work.tile([P, W], U8, align_bytes=64, name="mu_scales")
+            tiles[("q", rd)] = (mu_codes, mu_scales)
+            nc.vector.quantize_mx(
+                out=mu_codes[:].bitcast(FP8X4),
+                scales=mu_scales[:],
+                in_=mg[:].rearrange("p w t -> p (w t)"),
+            )
+
+        def second_mm(rd):
+            mu_codes, mu_scales = tiles[("q", rd)]
+            for cl in range(CG):
+                o_ps = pso.tile([P, CF], F32, tag="o", name="o_ps")
+                tiles[("o", rd, cl)] = o_ps
+                nc.tensor.matmul_mx(
+                    out=o_ps[:],
+                    lhsT=mu_codes[:, TOK * cl : TOK * (cl + 1)].bitcast(FP8X4),
+                    lhsT_scale=mu_scales[:, TOK * cl : TOK * (cl + 1)],
+                    rhs=w2_codes[:].bitcast(FP8X4),
+                    rhs_scale=w2_scales[:],
+                    start=True,
+                    stop=True,
+                )
+
+        def finish(rd, cls, lo=0, hi=CF):
+            if ("res", rd) not in tiles:
+                res_new = work.tile([P, CG, CF], F32, name="res")
+                tiles[("res", rd)] = res_new
+            res = tiles[("res", rd)]
+            for cl in cls:
+                nc.vector.tensor_tensor(
+                    out=res[:, cl, lo:hi],
+                    in0=tiles[("o", rd, cl)][:, lo:hi],
+                    in1=b2_bc[:, lo:hi],
+                    op=ALU.add,
+                )
+            for cl in cls:
+                nc.scalar.activation(out=res[:, cl, lo:hi], in_=res[:, cl, lo:hi], func=ACT.Tanh)
+            c0 = CG * rd + cls[0]
+            c1 = CG * rd + cls[-1] + 1
+            nc.sync.dma_start(
+                out=out3[:, c0:c1, lo:hi], in_=res[:, cls[0] : cls[-1] + 1, lo:hi]
+            )
+
+        for rd in range(LEAD + 1):
+            bcast_r(rd)
+        normalise(0, [0, 1, 2, 3])
+        gain_bias(0, [0, 1], "s")
+        gain_bias(0, [2, 3], "g")
+        load_b2()
+        normalise(1, [0, 1, 2, 3])
+        gain_bias(1, [2, 3], "g")
+        for rd in range(ROUNDS):
+            nxt = rd + LEAD
+            more = nxt < ROUNDS
+            if nxt + 1 < ROUNDS:
+                bcast_r(nxt + 1)
+            regroup_mu(rd, 256 if rd == ROUNDS - 1 else 0)
+            if rd == 0:
+                gain_bias(1, [0, 1], "s")
+            if more:
+                normalise(nxt, [0])
+            if rd > 0:
+                finish(rd - 1, [0, 1, 2, 3])
+            if more:
+                normalise(nxt, [1, 2])
+            quantise_mu(rd)
+            second_mm(rd)
+            if more:
+                normalise(nxt, [3])
+                if nxt == ROUNDS - 1:
+                    gain_bias(nxt, [0, 1], "v")
+                    gain_bias(nxt, [2, 3], "g")
+                else:
+                    gain_bias(nxt, [0, 1, 2, 3], "g")
+        last = ROUNDS - 1
+        finish(last, [0, 1])
+        finish(last, [2])
+        finish(last, [3], 0, CF // 2)
+        finish(last, [3], CF // 2, CF)

@@ -21,7 +21,6 @@ LN_EPS = 1e-5
 CG = 4
 ROUNDS = NCODE // CG
 W = CG * TOK
-LEAD = 2
 
 FLOPS = 2 * TOK * D_IN * CF + 2 * TOK * NCODE * CF * CF
 
@@ -30,6 +29,9 @@ ROW_G = 40
 ROW_B = 48
 ROW_B2 = 56
 W1_V = 352
+
+KINDS = ["gvee"] + ["ggee"] * 6 + ["gvee"]
+KB = [2, 2, 2, 2, 2, 2, 0, 0]
 
 
 def regroup(eng_copy, dst, src):
@@ -100,10 +102,14 @@ def tile_mixtureconfounderprior_pa_kernel(
         nc.vector.tensor_copy(
             out=hg[:].bitcast(F32), in_=xt[:].rearrange("p g u r -> p g r u")
         )
-        smT_ps = pso.tile([P, 4, P], BF16, tag="o")
+        smT_ps = pso.tile([P, 6, P], BF16, tag="o")
         for t in range(4):
             nc.tensor.transpose(smT_ps[:, t, :], sm_raw[:, t : CF : 4], ident_bf[:])
-        smT = keep.tile([P, 4, 64], F32)
+        for j in range(2):
+            nc.tensor.transpose(
+                smT_ps[:, 4 + j, :], sm_raw[:, P * (2 + j) : P * (3 + j)], ident_bf[:]
+            )
+        smT = keep.tile([P, 6, 64], F32)
         nc.scalar.copy(out=smT[:], in_=smT_ps[:, :, 0:64])
 
         w1g = keep.tile([P, 2, CF, 4], BF16, align_bytes=64)
@@ -122,10 +128,16 @@ def tile_mixtureconfounderprior_pa_kernel(
         cm1 = keep.tile([P, 4, NCODE], F32)
         nc.vector.tensor_tensor(
             out=cm1[:],
-            in0=smT[:, :, 0:NCODE],
-            in1=smT[:, :, ROW_B1 : ROW_B1 + 1].to_broadcast([P, 4, NCODE]),
+            in0=smT[:, 0:4, 0:NCODE],
+            in1=smT[:, 0:4, ROW_B1 : ROW_B1 + 1].to_broadcast([P, 4, NCODE]),
             op=ALU.add,
         )
+        neg_g = keep.tile([P, 4], F32)
+        nc.gpsimd.tensor_scalar(
+            out=neg_g[:], in0=smT[:, 0:4, ROW_G], scalar1=-1.0, scalar2=0.0, op0=ALU.mult, op1=ALU.add
+        )
+        b_col = keep.tile([P, 4], F32)
+        nc.gpsimd.tensor_copy(out=b_col[:], in_=smT[:, 0:4, ROW_B])
         cms = keep.tile([P, NCODE], F32)
         nc.vector.tensor_reduce(
             out=cms[:], in_=cm1[:].rearrange("p t c -> p c t"), axis=AX.X, op=ALU.add
@@ -144,6 +156,19 @@ def tile_mixtureconfounderprior_pa_kernel(
             scales=w1_scales[:, 1, :],
             in_=w1g[:, 1].rearrange("p c t -> p (c t)"),
         )
+
+        b_bc = keep.tile([P, CF], F32)
+        b2_bc = keep.tile([P, CF], F32)
+        for dst, row in ((b_bc, ROW_B), (b2_bc, ROW_B2)):
+            row_ps = psr.tile([P, CF], F32, tag="r", name="row_ps")
+            nc.tensor.matmul(
+                row_ps[:],
+                lhsT=ident_bf[:, row : row + 1].to_broadcast([P, P]),
+                rhs=sm_raw[:],
+                start=True,
+                stop=True,
+            )
+            nc.scalar.copy(out=dst[:], in_=row_ps[:])
 
         hpT_ps = [pso.tile([P, TOK], F32, tag="o", name="hpT_ps%d" % t) for t in range(4)]
         hp_ps = pso.tile([P, CF], F32, tag="o")
@@ -174,6 +199,13 @@ def tile_mixtureconfounderprior_pa_kernel(
             in1=mc_ps[:].unsqueeze(1).to_broadcast([P, 4, NCODE]),
             op=ALU.subtract,
         )
+        cg = keep.tile([P, 4, NCODE], F32)
+        nc.gpsimd.tensor_tensor(
+            out=cg[:],
+            in0=c_sb[:],
+            in1=smT[:, 0:4, ROW_G : ROW_G + 1].to_broadcast([P, 4, NCODE]),
+            op=ALU.mult,
+        )
         c2 = keep.tile([P, 4, NCODE], F32)
         nc.vector.tensor_scalar_mul(out=c2[:], in0=c_sb[:], scalar1=2.0 / CF)
         csq = keep.tile([P, 4, NCODE], F32)
@@ -183,14 +215,23 @@ def tile_mixtureconfounderprior_pa_kernel(
             out=cvs[:], in_=csq[:].rearrange("p t c -> p c t"), axis=AX.X, op=ALU.add
         )
         w2g = keep.tile([P, CF, 4], BF16, align_bytes=64)
-        regroup(nc.scalar.copy, w2g[:, 0 : CF // 2], w2_raw[:, :, 0 : CF // 2])
         hpT_v = keep.tile([P, 2, TOK], F32)
         hpT_s = keep.tile([P, 2, TOK], F32)
         for i in range(2):
             nc.vector.tensor_copy(out=hpT_v[:, i, :], in_=hpT_ps[i][:])
             nc.scalar.copy(out=hpT_s[:, i, :], in_=hpT_ps[2 + i][:])
+        hpTg = keep.tile([P, 4, TOK], F32)
+        for t in range(4):
+            nc.gpsimd.tensor_scalar(
+                out=hpTg[:, t, :],
+                in0=hpT_v[:, t, :] if t < 2 else hpT_s[:, t - 2, :],
+                scalar1=smT[:, t, ROW_G : ROW_G + 1],
+                scalar2=0.0,
+                op0=ALU.mult,
+                op1=ALU.add,
+            )
         hpT = [hpT_v[:, 0, :], hpT_v[:, 1, :], hpT_s[:, 0, :], hpT_s[:, 1, :]]
-        regroup(nc.scalar.copy, w2g[:, CF // 2 : CF], w2_raw[:, :, CF // 2 : CF])
+        regroup(nc.scalar.copy, w2g[:, 0 : CF // 2], w2_raw[:, :, 0 : CF // 2])
         v_ps = pso.tile([P, NCODE], F32, tag="o")
         nc.tensor.matmul(v_ps[:], lhsT=ones[:], rhs=cvs[:], start=True, stop=False)
         for t in range(4):
@@ -207,189 +248,278 @@ def tile_mixtureconfounderprior_pa_kernel(
         std = keep.tile([P, NCODE], F32)
         nc.scalar.activation(out=std[:], in_=v_ps[:], func=ACT.Sqrt, bias=vhe[:, 0:1])
         nc.scalar.activation(out=warm[:], in_=eps[:], func=ACT.Tanh)
+        regroup(nc.scalar.copy, w2g[:, CF // 2 : CF], w2_raw[:, :, CF // 2 : CF])
         w2_codes = keep.tile([P, CF], U32, align_bytes=64)
         w2_scales = keep.tile([P, CF], U8, align_bytes=64)
-        nc.vector.quantize_mx(
-            out=w2_codes[:].bitcast(FP8X4),
-            scales=w2_scales[:],
-            in_=w2g[:].rearrange("p c t -> p (c t)"),
-        )
         r_sb = keep.tile([P, NCODE], F32)
         nc.vector.reciprocal(out=r_sb[:], in_=std[:])
         a_sb = keep.tile([P, 4, TOK], F32)
-        nc.vector.tensor_tensor(
-            out=a_sb[:, 0:2, :],
-            in0=hpT_v[:],
-            in1=mh_ps[:].unsqueeze(1).to_broadcast([P, 2, TOK]),
-            op=ALU.subtract,
-        )
-        nc.vector.tensor_tensor(
-            out=a_sb[:, 2:4, :],
-            in0=hpT_s[:],
-            in1=mh_ps[:].unsqueeze(1).to_broadcast([P, 2, TOK]),
-            op=ALU.subtract,
-        )
-        b2_bc = keep.tile([P, CF], F32)
+        for t in range(4):
+            nc.vector.scalar_tensor_tensor(
+                out=a_sb[:, t, :],
+                in0=mh_ps[:],
+                scalar=neg_g[:, t : t + 1],
+                in1=hpTg[:, t, :],
+                op0=ALU.mult,
+                op1=ALU.add,
+            )
 
         tiles = {}
 
+        def codes_of(rd, kinds):
+            return [cl for cl in range(CG) if KINDS[rd][cl] in kinds]
+
         def bcast_r(rd):
-            for cl in range(CG):
+            cls = codes_of(rd, "gv")
+            if rd > 0 and cls:
+                r_ps = psr.tile([P, CG, TOK], F32, tag="r", name="r_ps")
+                tiles[("rt", rd)] = r_ps
+            for i, cl in enumerate(cls):
                 code = CG * rd + cl
                 if rd == 0:
                     r_one = pso.tile([P, TOK], F32, tag="o", name="r_one")
                     tiles[("r", rd, cl)] = r_one[:]
                 else:
-                    if cl == 0:
-                        r_ps = psr.tile([P, CG, TOK], F32, tag="r", name="r_ps")
-                        tiles[("rt", rd)] = r_ps
-                    tiles[("r", rd, cl)] = tiles[("rt", rd)][:, cl, :]
+                    tiles[("r", rd, cl)] = tiles[("rt", rd)][:, i, :]
                 nc.tensor.transpose(
                     tiles[("r", rd, cl)], r_sb[:, code : code + 1].to_broadcast([P, P]), ident[:]
                 )
 
-        def load_b2():
-            b2_ps = pso.tile([P, CF], F32, tag="o", name="b2_ps")
-            nc.tensor.matmul(
-                b2_ps[:],
-                lhsT=ident_bf[:, ROW_B2 : ROW_B2 + 1].to_broadcast([P, P]),
-                rhs=sm_raw[:],
-                start=True,
-                stop=True,
-            )
-            nc.scalar.copy(out=b2_bc[:], in_=b2_ps[:])
-
-        def normalise(rd, cls):
-            if cls[0] == 0:
-                z_new = work.tile([P, 4, CG, TOK], F32, name="z")
-                tiles[("z", rd)] = z_new
-            z = tiles[("z", rd)]
-            for cl in cls:
+        def normalise(rd):
+            z = work.tile([P, 4, CG, TOK], F32, name="z")
+            tiles[("z", rd)] = z
+            for cl in codes_of(rd, "gv"):
                 code = CG * rd + cl
                 for t in range(4):
                     nc.vector.scalar_tensor_tensor(
                         out=z[:, t, cl, :],
                         in0=a_sb[:, t, :],
-                        scalar=c_sb[:, t, code : code + 1],
+                        scalar=cg[:, t, code : code + 1],
                         in1=tiles[("r", rd, cl)],
                         op0=ALU.add,
                         op1=ALU.mult,
                     )
 
-        def gain_bias(rd, planes, eng):
+        def mg_of(rd):
+            if ("mg", rd) not in tiles:
+                mg = work.tile([P, W, 4], BF16, align_bytes=64, name="mg")
+                tiles[("mg", rd)] = mg
+            return tiles[("mg", rd)]
+
+        def add_bias(rd, kind):
             z = tiles[("z", rd)]
-            if ("m", rd) not in tiles:
-                m_new = work.tile([P, 4, W], BF16, name="m")
-                tiles[("m", rd)] = m_new
-            m = tiles[("m", rd)]
-            for t in planes:
-                if eng == "s":
-                    nc.scalar.activation(
-                        out=m[:, t, :],
-                        in_=z[:, t].rearrange("p c r -> p (c r)"),
-                        func=ACT.Identity,
-                        scale=smT[:, t, ROW_G : ROW_G + 1],
-                        bias=smT[:, t, ROW_B : ROW_B + 1],
+            engine = nc.gpsimd if kind == "g" else nc.vector
+            for cl in codes_of(rd, kind):
+                engine.tensor_tensor(
+                    out=mg_of(rd)[:, TOK * cl : TOK * (cl + 1), :].rearrange(
+                        "p (c i) t -> p c t i", i=4
+                    ),
+                    in0=z[:, :, cl, :].rearrange("p t (c i) -> p c t i", i=4),
+                    in1=b_col[:].unsqueeze(1).unsqueeze(3).to_broadcast([P, TOK // 4, 4, 4]),
+                    op=ALU.add,
+                )
+
+        def sum_rows(rd):
+            for cl in codes_of(rd, "e"):
+                code = CG * rd + cl
+                u = pso.tile([P, 4, P], F32, tag="o", name="u")
+                tiles[("u", rd, cl)] = u
+                for t in range(4):
+                    nc.tensor.matmul(
+                        u[:, t, :], lhsT=a_sb[:, t, :], rhs=ident[:], start=True, stop=False, is_transpose=True
                     )
-                else:
-                    engine = nc.gpsimd if eng == "g" else nc.vector
-                    engine.tensor_scalar(
-                        out=m[:, t, :],
-                        in0=z[:, t].rearrange("p c r -> p (c r)"),
-                        scalar1=smT[:, t, ROW_G : ROW_G + 1],
-                        scalar2=smT[:, t, ROW_B : ROW_B + 1],
-                        op0=ALU.mult,
-                        op1=ALU.add,
+                    nc.tensor.matmul(
+                        u[:, t, :],
+                        lhsT=cg[:, t, code : code + 1].to_broadcast([P, P]),
+                        rhs=ident[:],
+                        start=False,
+                        stop=True,
+                        is_transpose=True,
                     )
 
-        def regroup_mu(rd, rv):
-            m = tiles[("m", rd)]
-            mg = work.tile([P, W, 4], BF16, align_bytes=64, name="mg")
-            tiles[("mg", rd)] = mg
-            if rv > 0:
-                regroup(nc.vector.tensor_copy, mg[:, 0:rv], m[:, :, 0:rv])
-            if rv < W:
-                regroup(nc.scalar.copy, mg[:, rv:W], m[:, :, rv:W])
+        def scale_rows(rd):
+            for cl in codes_of(rd, "e"):
+                code = CG * rd + cl
+                x = work.tile([P, CF], BF16, name="x")
+                tiles[("x", rd, cl)] = x
+                nc.vector.scalar_tensor_tensor(
+                    out=x[:].rearrange("p (r t) -> p r t", t=4),
+                    in0=tiles[("u", rd, cl)][:].rearrange("p t r -> p r t"),
+                    scalar=r_sb[:, code : code + 1],
+                    in1=b_bc[:].rearrange("p (r t) -> p r t", t=4),
+                    op0=ALU.mult,
+                    op1=ALU.add,
+                )
+
+        def turn_rows(rd):
+            cls = codes_of(rd, "e")
+            xt_ps = pso.tile([P, len(cls), 2, TOK], F32, tag="o", name="xt_ps")
+            tiles[("xt", rd)] = xt_ps
+            for i, cl in enumerate(cls):
+                words = tiles[("x", rd, cl)][:].bitcast(F32)
+                for u in range(2):
+                    nc.tensor.transpose(xt_ps[:, i, u, :], words[:, u : CF // 2 : 2], ident[:])
+
+        def copy_rows(rd):
+            cls = codes_of(rd, "e")
+            part = mg_of(rd)[:, TOK * cls[0] : TOK * (cls[-1] + 1), :].bitcast(F32)
+            nc.scalar.copy(
+                out=part.rearrange("p (c r) u -> p c r u", r=TOK),
+                in_=tiles[("xt", rd)][:].rearrange("p c u r -> p c r u"),
+            )
 
         def quantise_mu(rd):
-            mg = tiles[("mg", rd)]
             mu_codes = work.tile([P, W], U32, align_bytes=64, name="mu_codes")
             mu_scales = work.tile([P, W], U8, align_bytes=64, name="mu_scales")
             tiles[("q", rd)] = (mu_codes, mu_scales)
             nc.vector.quantize_mx(
                 out=mu_codes[:].bitcast(FP8X4),
                 scales=mu_scales[:],
-                in_=mg[:].rearrange("p w t -> p (w t)"),
+                in_=mg_of(rd)[:].rearrange("p w t -> p (w t)"),
             )
 
         def second_mm(rd):
             mu_codes, mu_scales = tiles[("q", rd)]
-            for cl in range(CG):
-                o_ps = pso.tile([P, CF], F32, tag="o", name="o_ps")
-                tiles[("o", rd, cl)] = o_ps
+            res = work.tile([P, CG, CF], F32, name="res")
+            tiles[("res", rd)] = res
+            kb = KB[rd]
+            wa = CF - P * kb
+            for nb in range(CF // P - kb, CF // P):
+                o_ps = pso.tile([P, W], F32, tag="o", name="ob_ps")
+                tiles[("ob", rd, nb)] = o_ps
                 nc.tensor.matmul_mx(
                     out=o_ps[:],
-                    lhsT=mu_codes[:, TOK * cl : TOK * (cl + 1)].bitcast(FP8X4),
-                    lhsT_scale=mu_scales[:, TOK * cl : TOK * (cl + 1)],
-                    rhs=w2_codes[:].bitcast(FP8X4),
-                    rhs_scale=w2_scales[:],
+                    lhsT=w2_codes[:, P * nb : P * (nb + 1)].bitcast(FP8X4),
+                    lhsT_scale=w2_scales[:, P * nb : P * (nb + 1)],
+                    rhs=mu_codes[:].bitcast(FP8X4),
+                    rhs_scale=mu_scales[:],
                     start=True,
                     stop=True,
                 )
+            per = CF // wa
+            for c0 in range(0, CG, per):
+                o_ps = pso.tile([P, per, wa], F32, tag="o", name="oa_ps")
+                tiles[("oa", rd, c0)] = o_ps
+                for i in range(per):
+                    cl = c0 + i
+                    nc.tensor.matmul_mx(
+                        out=o_ps[:, i, :],
+                        lhsT=mu_codes[:, TOK * cl : TOK * (cl + 1)].bitcast(FP8X4),
+                        lhsT_scale=mu_scales[:, TOK * cl : TOK * (cl + 1)],
+                        rhs=w2_codes[:, 0:wa].bitcast(FP8X4),
+                        rhs_scale=w2_scales[:, 0:wa],
+                        start=True,
+                        stop=True,
+                    )
 
-        def finish(rd, cls, lo=0, hi=CF):
-            if ("res", rd) not in tiles:
-                res_new = work.tile([P, CG, CF], F32, name="res")
-                tiles[("res", rd)] = res_new
-            res = tiles[("res", rd)]
-            for cl in cls:
-                nc.vector.tensor_tensor(
-                    out=res[:, cl, lo:hi],
-                    in0=tiles[("o", rd, cl)][:, lo:hi],
-                    in1=b2_bc[:, lo:hi],
-                    op=ALU.add,
+        def tanh_b(rd):
+            for nb in range(CF // P - KB[rd], CF // P):
+                th = work.tile([P, W], F32, name="th")
+                tiles[("th", rd, nb)] = th
+                nc.scalar.activation(
+                    out=th[:],
+                    in_=tiles[("ob", rd, nb)][:],
+                    func=ACT.Tanh,
+                    bias=smT[:, 2 + nb, ROW_B2 : ROW_B2 + 1],
                 )
-            for cl in cls:
-                nc.scalar.activation(out=res[:, cl, lo:hi], in_=res[:, cl, lo:hi], func=ACT.Tanh)
-            c0 = CG * rd + cls[0]
-            c1 = CG * rd + cls[-1] + 1
-            nc.sync.dma_start(
-                out=out3[:, c0:c1, lo:hi], in_=res[:, cls[0] : cls[-1] + 1, lo:hi]
+
+        def turn_b(rd):
+            for nb in range(CF // P - KB[rd], CF // P):
+                tr = pso.tile([P, CG, P], F32, tag="o", name="tr")
+                tiles[("tr", rd, nb)] = tr
+                for cl in range(CG):
+                    nc.tensor.transpose(
+                        tr[:, cl, :], tiles[("th", rd, nb)][:, TOK * cl : TOK * (cl + 1)], ident[:]
+                    )
+
+        def copy_b(rd):
+            for nb in range(CF // P - KB[rd], CF // P):
+                nc.scalar.copy(
+                    out=tiles[("res", rd)][:, :, P * nb : P * (nb + 1)], in_=tiles[("tr", rd, nb)][:]
+                )
+
+        def add_a(rd, c0, lo=0, hi=CF):
+            o_ps = tiles[("oa", rd, c0)]
+            wa = CF - P * KB[rd]
+            hi = min(hi, wa)
+            per = CF // wa
+            nc.vector.tensor_tensor(
+                out=tiles[("res", rd)][:, c0 : c0 + per, lo:hi],
+                in0=o_ps[:, :, lo:hi],
+                in1=b2_bc[:, lo:hi].unsqueeze(1).to_broadcast([P, per, hi - lo]),
+                op=ALU.add,
             )
 
-        for rd in range(LEAD + 1):
-            bcast_r(rd)
-        normalise(0, [0, 1, 2, 3])
-        gain_bias(0, [0, 1], "s")
-        gain_bias(0, [2, 3], "g")
-        load_b2()
-        normalise(1, [0, 1, 2, 3])
-        gain_bias(1, [2, 3], "g")
+        def tanh_a(rd, c0, lo=0, hi=CF):
+            wa = CF - P * KB[rd]
+            hi = min(hi, wa)
+            part = tiles[("res", rd)][:, c0 : c0 + CF // wa, lo:hi]
+            nc.scalar.activation(out=part, in_=part, func=ACT.Tanh)
+
+        def store(rd, c0, c1, lo=0, hi=CF):
+            nc.sync.dma_start(
+                out=out3[:, CG * rd + c0 : CG * rd + c1, lo:hi],
+                in_=tiles[("res", rd)][:, c0:c1, lo:hi],
+            )
+
+        def a_groups(rd):
+            return range(0, CG, CF // (CF - P * KB[rd]))
+
+        bcast_r(0)
+        sum_rows(0)
+        normalise(0)
+        add_bias(0, "g")
+        scale_rows(0)
+        add_bias(0, "v")
+        bcast_r(1)
+        turn_rows(0)
+        copy_rows(0)
+        sum_rows(1)
+        bcast_r(2)
+        nc.vector.quantize_mx(
+            out=w2_codes[:].bitcast(FP8X4),
+            scales=w2_scales[:],
+            in_=w2g[:].rearrange("p c t -> p (c t)"),
+        )
+        normalise(1)
+        scale_rows(1)
+        turn_rows(1)
+        last = ROUNDS - 1
         for rd in range(ROUNDS):
-            nxt = rd + LEAD
-            more = nxt < ROUNDS
-            if nxt + 1 < ROUNDS:
-                bcast_r(nxt + 1)
-            regroup_mu(rd, 256 if rd == ROUNDS - 1 else 0)
-            if rd == 0:
-                gain_bias(1, [0, 1], "s")
-            if more:
-                normalise(nxt, [0])
-            if rd > 0:
-                finish(rd - 1, [0, 1, 2, 3])
-            if more:
-                normalise(nxt, [1, 2])
             quantise_mu(rd)
             second_mm(rd)
-            if more:
-                normalise(nxt, [3])
-                if nxt == ROUNDS - 1:
-                    gain_bias(nxt, [0, 1], "v")
-                    gain_bias(nxt, [2, 3], "g")
-                else:
-                    gain_bias(nxt, [0, 1, 2, 3], "g")
-        last = ROUNDS - 1
-        finish(last, [0, 1])
-        finish(last, [2])
-        finish(last, [3], 0, CF // 2)
-        finish(last, [3], CF // 2, CF)
+            if rd + 3 < ROUNDS:
+                bcast_r(rd + 3)
+            if rd + 2 < ROUNDS:
+                sum_rows(rd + 2)
+            if rd + 1 < ROUNDS:
+                add_bias(rd + 1, "g")
+                add_bias(rd + 1, "v")
+            if rd + 2 < ROUNDS:
+                normalise(rd + 2)
+            if rd > 0:
+                copy_b(rd - 1)
+                store(rd - 1, 0, CG)
+            if rd + 1 < ROUNDS:
+                copy_rows(rd + 1)
+            if rd == last:
+                break
+            tanh_b(rd)
+            turn_b(rd)
+            for c0 in a_groups(rd):
+                add_a(rd, c0)
+            for c0 in a_groups(rd):
+                tanh_a(rd, c0)
+            if rd + 2 < ROUNDS:
+                scale_rows(rd + 2)
+                turn_rows(rd + 2)
+        for c0 in range(CG - 1):
+            add_a(last, c0)
+        for c0 in range(CG - 1):
+            tanh_a(last, c0)
+            if c0 > 0:
+                store(last, 0 if c0 == 1 else c0, c0 + 1)
+        for lo in (0, CF // 2):
+            add_a(last, CG - 1, lo, lo + CF // 2)
+            tanh_a(last, CG - 1, lo, lo + CF // 2)
+            store(last, CG - 1, CG, lo, lo + CF // 2)

@@ -28,7 +28,7 @@ ROW_B1 = 32
 ROW_G = 40
 ROW_B = 48
 ROW_B2 = 56
-W1_V = 352
+W1_V = 320
 
 KINDS = ["gvee"] + ["ggee"] * 6 + ["gvee"]
 KB = [2, 2, 2, 2, 2, 2, 0, 0]
@@ -86,6 +86,8 @@ def tile_mixtureconfounderprior_pa_kernel(
         make_identity(nc, ident_bf[:])
         ones = keep.tile([P, P], F32)
         nc.vector.memset(ones[:], 1.0 / CF)
+        halves = keep.tile([P, P], F32)
+        nc.vector.memset(halves[:], 0.5)
         eps = keep.tile([P, 1], F32)
         nc.vector.memset(eps[:], LN_EPS)
         warm = keep.tile([P, 1], F32)
@@ -99,9 +101,7 @@ def tile_mixtureconfounderprior_pa_kernel(
                     xt[:, g, u, :], h_w[:, 256 * g + u : 256 * (g + 1) : 2], ident[:]
                 )
         hg = keep.tile([P, 2, TOK, 4], BF16, align_bytes=64)
-        nc.vector.tensor_copy(
-            out=hg[:].bitcast(F32), in_=xt[:].rearrange("p g u r -> p g r u")
-        )
+        nc.scalar.copy(out=hg[:].bitcast(F32), in_=xt[:].rearrange("p g u r -> p g r u"))
         smT_ps = pso.tile([P, 6, P], BF16, tag="o")
         for t in range(4):
             nc.tensor.transpose(smT_ps[:, t, :], sm_raw[:, t : CF : 4], ident_bf[:])
@@ -109,14 +109,30 @@ def tile_mixtureconfounderprior_pa_kernel(
             nc.tensor.transpose(
                 smT_ps[:, 4 + j, :], sm_raw[:, P * (2 + j) : P * (3 + j)], ident_bf[:]
             )
-        smT = keep.tile([P, 6, 64], F32)
-        nc.scalar.copy(out=smT[:], in_=smT_ps[:, :, 0:64])
+        rows_ps = []
+        for row in (ROW_B, ROW_B2):
+            row_ps = psr.tile([P, CF], F32, tag="r", name="row_ps")
+            rows_ps.append(row_ps)
+            nc.tensor.matmul(
+                row_ps[:],
+                lhsT=ident_bf[:, row : row + 1].to_broadcast([P, P]),
+                rhs=sm_raw[:],
+                start=True,
+                stop=True,
+            )
 
         w1g = keep.tile([P, 2, CF, 4], BF16, align_bytes=64)
         w1_codes = keep.tile([P, 2, CF], U32, align_bytes=64)
         w1_scales = keep.tile([P, 2, CF], U8, align_bytes=64)
         h_codes = keep.tile([P, 2 * TOK], U32, align_bytes=64)
         h_scales = keep.tile([P, 2 * TOK], U8, align_bytes=64)
+
+        def quantise_w1(g):
+            nc.vector.quantize_mx(
+                out=w1_codes[:, g, :].bitcast(FP8X4),
+                scales=w1_scales[:, g, :],
+                in_=w1g[:, g].rearrange("p c t -> p (c t)"),
+            )
 
         regroup_w1(nc.vector.tensor_copy, w1g[:, 0], w1_raw[:, 0], 0, W1_V // 4)
         regroup_w1(nc.scalar.copy, w1g[:, 0], w1_raw[:, 0], W1_V // 4, P)
@@ -125,50 +141,10 @@ def tile_mixtureconfounderprior_pa_kernel(
             scales=h_scales[:],
             in_=hg[:].rearrange("p g r t -> p (g r t)"),
         )
-        cm1 = keep.tile([P, 4, NCODE], F32)
-        nc.vector.tensor_tensor(
-            out=cm1[:],
-            in0=smT[:, 0:4, 0:NCODE],
-            in1=smT[:, 0:4, ROW_B1 : ROW_B1 + 1].to_broadcast([P, 4, NCODE]),
-            op=ALU.add,
-        )
-        neg_g = keep.tile([P, 4], F32)
-        nc.gpsimd.tensor_scalar(
-            out=neg_g[:], in0=smT[:, 0:4, ROW_G], scalar1=-1.0, scalar2=0.0, op0=ALU.mult, op1=ALU.add
-        )
-        b_col = keep.tile([P, 4], F32)
-        nc.gpsimd.tensor_copy(out=b_col[:], in_=smT[:, 0:4, ROW_B])
-        cms = keep.tile([P, NCODE], F32)
-        nc.vector.tensor_reduce(
-            out=cms[:], in_=cm1[:].rearrange("p t c -> p c t"), axis=AX.X, op=ALU.add
-        )
-        mc_ps = pso.tile([P, NCODE], F32, tag="o")
-        nc.tensor.matmul(mc_ps[:], lhsT=ones[:], rhs=cms[:], start=True, stop=True)
-        nc.vector.quantize_mx(
-            out=w1_codes[:, 0, :].bitcast(FP8X4),
-            scales=w1_scales[:, 0, :],
-            in_=w1g[:, 0].rearrange("p c t -> p (c t)"),
-        )
+        quantise_w1(0)
         regroup_w1(nc.vector.tensor_copy, w1g[:, 1], w1_raw[:, 1], 0, W1_V // 4)
         regroup_w1(nc.scalar.copy, w1g[:, 1], w1_raw[:, 1], W1_V // 4, P)
-        nc.vector.quantize_mx(
-            out=w1_codes[:, 1, :].bitcast(FP8X4),
-            scales=w1_scales[:, 1, :],
-            in_=w1g[:, 1].rearrange("p c t -> p (c t)"),
-        )
-
-        b_bc = keep.tile([P, CF], F32)
-        b2_bc = keep.tile([P, CF], F32)
-        for dst, row in ((b_bc, ROW_B), (b2_bc, ROW_B2)):
-            row_ps = psr.tile([P, CF], F32, tag="r", name="row_ps")
-            nc.tensor.matmul(
-                row_ps[:],
-                lhsT=ident_bf[:, row : row + 1].to_broadcast([P, P]),
-                rhs=sm_raw[:],
-                start=True,
-                stop=True,
-            )
-            nc.scalar.copy(out=dst[:], in_=row_ps[:])
+        quantise_w1(1)
 
         hpT_ps = [pso.tile([P, TOK], F32, tag="o", name="hpT_ps%d" % t) for t in range(4)]
         hp_ps = pso.tile([P, CF], F32, tag="o")
@@ -192,6 +168,38 @@ def tile_mixtureconfounderprior_pa_kernel(
                 start=(g == 0),
                 stop=(g == 1),
             )
+
+        smT = keep.tile([P, 6, 64], F32)
+        nc.scalar.copy(out=smT[:], in_=smT_ps[:, :, 0:64])
+        cm1 = keep.tile([P, 4, NCODE], F32)
+        nc.vector.tensor_tensor(
+            out=cm1[:],
+            in0=smT[:, 0:4, 0:NCODE],
+            in1=smT[:, 0:4, ROW_B1 : ROW_B1 + 1].to_broadcast([P, 4, NCODE]),
+            op=ALU.add,
+        )
+        neg_g = keep.tile([P, 4], F32)
+        nc.gpsimd.tensor_scalar(
+            out=neg_g[:], in0=smT[:, 0:4, ROW_G], scalar1=-1.0, scalar2=0.0, op0=ALU.mult, op1=ALU.add
+        )
+        b_col = keep.tile([P, 4], F32)
+        nc.gpsimd.tensor_copy(out=b_col[:], in_=smT[:, 0:4, ROW_B])
+        cms = keep.tile([P, NCODE], F32)
+        nc.vector.tensor_reduce(
+            out=cms[:], in_=cm1[:].rearrange("p t c -> p c t"), axis=AX.X, op=ALU.add
+        )
+        b_bc = keep.tile([P, CF], F32)
+        b2_bc = keep.tile([P, CF], F32)
+        nc.scalar.copy(out=b_bc[:], in_=rows_ps[0][:])
+        nc.scalar.copy(out=b2_bc[:], in_=rows_ps[1][:])
+        mc_ps = pso.tile([P, NCODE], F32, tag="o")
+        nc.tensor.matmul(mc_ps[:], lhsT=ones[:], rhs=cms[:], start=True, stop=True)
+        hpT_v = keep.tile([P, 2, TOK], F32)
+        hpT_s = keep.tile([P, 2, TOK], F32)
+        for i in range(2):
+            nc.vector.tensor_copy(out=hpT_v[:, i, :], in_=hpT_ps[i][:])
+            nc.scalar.copy(out=hpT_s[:, i, :], in_=hpT_ps[2 + i][:])
+        hpT = [hpT_v[:, 0, :], hpT_v[:, 1, :], hpT_s[:, 0, :], hpT_s[:, 1, :]]
         c_sb = keep.tile([P, 4, NCODE], F32)
         nc.vector.tensor_tensor(
             out=c_sb[:],
@@ -199,6 +207,22 @@ def tile_mixtureconfounderprior_pa_kernel(
             in1=mc_ps[:].unsqueeze(1).to_broadcast([P, 4, NCODE]),
             op=ALU.subtract,
         )
+        csq = keep.tile([P, 4, NCODE], F32)
+        nc.vector.tensor_tensor(out=csq[:], in0=c_sb[:], in1=c_sb[:], op=ALU.mult)
+        cvs = keep.tile([P, NCODE], F32)
+        nc.vector.tensor_reduce(
+            out=cvs[:], in_=csq[:].rearrange("p t c -> p c t"), axis=AX.X, op=ALU.add
+        )
+        hpTg = keep.tile([P, 4, TOK], F32)
+        for t in range(4):
+            nc.gpsimd.tensor_scalar(
+                out=hpTg[:, t, :],
+                in0=hpT[t],
+                scalar1=smT[:, t, ROW_G : ROW_G + 1],
+                scalar2=0.0,
+                op0=ALU.mult,
+                op1=ALU.add,
+            )
         cg = keep.tile([P, 4, NCODE], F32)
         nc.gpsimd.tensor_tensor(
             out=cg[:],
@@ -206,37 +230,13 @@ def tile_mixtureconfounderprior_pa_kernel(
             in1=smT[:, 0:4, ROW_G : ROW_G + 1].to_broadcast([P, 4, NCODE]),
             op=ALU.mult,
         )
-        c2 = keep.tile([P, 4, NCODE], F32)
-        nc.vector.tensor_scalar_mul(out=c2[:], in0=c_sb[:], scalar1=2.0 / CF)
-        csq = keep.tile([P, 4, NCODE], F32)
-        nc.vector.tensor_tensor(out=csq[:], in0=c_sb[:], in1=c_sb[:], op=ALU.mult)
-        cvs = keep.tile([P, NCODE], F32)
-        nc.vector.tensor_reduce(
-            out=cvs[:], in_=csq[:].rearrange("p t c -> p c t"), axis=AX.X, op=ALU.add
-        )
         w2g = keep.tile([P, CF, 4], BF16, align_bytes=64)
-        hpT_v = keep.tile([P, 2, TOK], F32)
-        hpT_s = keep.tile([P, 2, TOK], F32)
-        for i in range(2):
-            nc.vector.tensor_copy(out=hpT_v[:, i, :], in_=hpT_ps[i][:])
-            nc.scalar.copy(out=hpT_s[:, i, :], in_=hpT_ps[2 + i][:])
-        hpTg = keep.tile([P, 4, TOK], F32)
-        for t in range(4):
-            nc.gpsimd.tensor_scalar(
-                out=hpTg[:, t, :],
-                in0=hpT_v[:, t, :] if t < 2 else hpT_s[:, t - 2, :],
-                scalar1=smT[:, t, ROW_G : ROW_G + 1],
-                scalar2=0.0,
-                op0=ALU.mult,
-                op1=ALU.add,
-            )
-        hpT = [hpT_v[:, 0, :], hpT_v[:, 1, :], hpT_s[:, 0, :], hpT_s[:, 1, :]]
         regroup(nc.scalar.copy, w2g[:, 0 : CF // 2], w2_raw[:, :, 0 : CF // 2])
-        v_ps = pso.tile([P, NCODE], F32, tag="o")
-        nc.tensor.matmul(v_ps[:], lhsT=ones[:], rhs=cvs[:], start=True, stop=False)
-        for t in range(4):
-            nc.tensor.matmul(v_ps[:], lhsT=hpT[t], rhs=c2[:, t, :], start=False, stop=(t == 3))
 
+        v_ps = pso.tile([P, NCODE], F32, tag="o")
+        for t in range(4):
+            nc.tensor.matmul(v_ps[:], lhsT=hpT[t], rhs=c_sb[:, t, :], start=(t == 0), stop=False)
+        nc.tensor.matmul(v_ps[:], lhsT=halves[:], rhs=cvs[:], start=False, stop=True)
         st = keep.tile([P, 6], F32)
         nc.vector.bn_stats(out=st[:], in_=hp_ps[:])
         mv = keep.tile([P, 2], F32)
@@ -246,13 +246,13 @@ def tile_mixtureconfounderprior_pa_kernel(
         mh_ps = pso.tile([P, TOK], F32, tag="o")
         nc.tensor.transpose(mh_ps[:], mv[:, 0:1].to_broadcast([P, P]), ident[:])
         std = keep.tile([P, NCODE], F32)
-        nc.scalar.activation(out=std[:], in_=v_ps[:], func=ACT.Sqrt, bias=vhe[:, 0:1])
+        nc.scalar.activation(
+            out=std[:], in_=v_ps[:], func=ACT.Sqrt, bias=vhe[:, 0:1], scale=2.0 / CF
+        )
         nc.scalar.activation(out=warm[:], in_=eps[:], func=ACT.Tanh)
         regroup(nc.scalar.copy, w2g[:, CF // 2 : CF], w2_raw[:, :, CF // 2 : CF])
         w2_codes = keep.tile([P, CF], U32, align_bytes=64)
         w2_scales = keep.tile([P, CF], U8, align_bytes=64)
-        r_sb = keep.tile([P, NCODE], F32)
-        nc.vector.reciprocal(out=r_sb[:], in_=std[:])
         a_sb = keep.tile([P, 4, TOK], F32)
         for t in range(4):
             nc.vector.scalar_tensor_tensor(
@@ -263,6 +263,8 @@ def tile_mixtureconfounderprior_pa_kernel(
                 op0=ALU.mult,
                 op1=ALU.add,
             )
+        r_sb = keep.tile([P, NCODE], F32)
+        nc.vector.reciprocal(out=r_sb[:], in_=std[:])
 
         tiles = {}
 
@@ -475,28 +477,23 @@ def tile_mixtureconfounderprior_pa_kernel(
         turn_rows(0)
         copy_rows(0)
         sum_rows(1)
-        bcast_r(2)
         nc.vector.quantize_mx(
             out=w2_codes[:].bitcast(FP8X4),
             scales=w2_scales[:],
             in_=w2g[:].rearrange("p c t -> p (c t)"),
         )
-        normalise(1)
         scale_rows(1)
         turn_rows(1)
         last = ROUNDS - 1
         for rd in range(ROUNDS):
             quantise_mu(rd)
             second_mm(rd)
-            if rd + 3 < ROUNDS:
-                bcast_r(rd + 3)
             if rd + 2 < ROUNDS:
+                bcast_r(rd + 2)
                 sum_rows(rd + 2)
             if rd + 1 < ROUNDS:
+                normalise(rd + 1)
                 add_bias(rd + 1, "g")
-                add_bias(rd + 1, "v")
-            if rd + 2 < ROUNDS:
-                normalise(rd + 2)
             if rd > 0:
                 copy_b(rd - 1)
                 store(rd - 1, 0, CG)
@@ -510,6 +507,7 @@ def tile_mixtureconfounderprior_pa_kernel(
                 add_a(rd, c0)
             for c0 in a_groups(rd):
                 tanh_a(rd, c0)
+            add_bias(rd + 1, "v")
             if rd + 2 < ROUNDS:
                 scale_rows(rd + 2)
                 turn_rows(rd + 2)

@@ -18,9 +18,6 @@ D_IN = 1024
 CF = 512
 NCODE = 32
 LN_EPS = 1e-5
-CG = 4
-ROUNDS = NCODE // CG
-W = CG * TOK
 
 FLOPS = 2 * TOK * D_IN * CF + 2 * TOK * NCODE * CF * CF
 
@@ -28,21 +25,34 @@ ROW_B1 = 32
 ROW_G = 40
 ROW_B = 48
 ROW_B2 = 56
-W1_V = 320
+W1_V = 288
+W1_V2 = 288
+D0 = 3
+D1 = 3
+D2 = 2
+DA = 4
+DB = 4
+DC = 2
+W2G = 2
+W2S = 2
 
-KINDS = ["gvee"] + ["ggee"] * 6 + ["gvee"]
-KB = [2, 2, 2, 2, 2, 2, 0, 0]
+
+KINDS = ["gv","ggee","ggee","ggee","ggee","ggee","ggee","ggee","gv"]
+KB = [0,2,2,2,2,2,2,0,0]
+FIRST = [sum(len(k) for k in KINDS[:i]) for i in range(len(KINDS))]
+ROUNDS = len(KINDS)
+BLK = 4
 
 
-def regroup(eng_copy, dst, src):
-    eng_copy(
+def regroup(op, dst, src):
+    op(
         out=dst.rearrange("p (c i) t -> p c t i", i=4),
         in_=src.rearrange("p t (c i) -> p c t i", i=4),
     )
 
 
-def regroup_w1(eng_copy, dst, src, m0, m1):
-    eng_copy(
+def regroup_w1(op, dst, src, m0, m1):
+    op(
         out=dst.rearrange("p (t m) j -> p t m j", t=4)[:, :, m0:m1],
         in_=src.rearrange("p j (m t) -> p t m j", t=4)[:, :, m0:m1],
     )
@@ -70,8 +80,6 @@ def tile_mixtureconfounderprior_pa_kernel(
                 out=w1_raw[:, g],
                 in_=mu_w1_h[512 * g : 512 * (g + 1), :].rearrange("(p j) c -> p j c", j=4),
             )
-        w2_raw = keep.tile([P, 4, CF], BF16)
-        nc.sync.dma_start(out=w2_raw[:], in_=mu_w2.rearrange("(p t) n -> p t n", t=4))
         sm_raw = keep.tile([P, CF], BF16)
         nc.scalar.dma_start(out=sm_raw[0:NCODE, :], in_=code_mu)
         nc.scalar.dma_start(out=sm_raw[ROW_B1 : ROW_B1 + 8, :], in_=mu_b1.partition_broadcast(8))
@@ -79,6 +87,8 @@ def tile_mixtureconfounderprior_pa_kernel(
         nc.scalar.dma_start(out=sm_raw[ROW_B : ROW_B + 8, :], in_=ln_b.partition_broadcast(8))
         nc.scalar.dma_start(out=sm_raw[ROW_B2 : ROW_B2 + 8, :], in_=mu_b2.partition_broadcast(8))
         nc.vector.memset(sm_raw[64:128, :].bitcast(F32), 0.0)
+        w2_raw = keep.tile([P, 4, CF], BF16)
+        nc.scalar.dma_start(out=w2_raw[:], in_=mu_w2.rearrange("(p t) n -> p t n", t=4))
 
         ident = keep.tile([P, P], F32)
         make_identity(nc, ident[:])
@@ -93,7 +103,13 @@ def tile_mixtureconfounderprior_pa_kernel(
         warm = keep.tile([P, 1], F32)
         nc.scalar.activation(out=warm[:], in_=eps[:], func=ACT.Sqrt)
 
+        def dummy(n):
+            busy = pso.tile([P, P], F32, tag="o", name="busy")
+            for i in range(n):
+                nc.tensor.matmul(busy[:], lhsT=ident[:], rhs=ident[:], start=True, stop=True)
+
         h_w = h_sb[:].bitcast(F32)
+        dummy(D0)
         xt = pso.tile([P, 2, 2, P], F32, tag="o")
         for g in range(2):
             for u in range(2):
@@ -142,13 +158,53 @@ def tile_mixtureconfounderprior_pa_kernel(
             in_=hg[:].rearrange("p g r t -> p (g r t)"),
         )
         quantise_w1(0)
-        regroup_w1(nc.vector.tensor_copy, w1g[:, 1], w1_raw[:, 1], 0, W1_V // 4)
-        regroup_w1(nc.scalar.copy, w1g[:, 1], w1_raw[:, 1], W1_V // 4, P)
+        regroup_w1(nc.vector.tensor_copy, w1g[:, 1], w1_raw[:, 1], 0, W1_V2 // 4)
+        regroup_w1(nc.scalar.copy, w1g[:, 1], w1_raw[:, 1], W1_V2 // 4, P)
+        smT = keep.tile([P, 6, 64], F32)
+        nc.scalar.copy(out=smT[:], in_=smT_ps[:, :, 0:64])
+        b_bc = keep.tile([P, CF], F32)
+        b2_bc = keep.tile([P, CF], F32)
+        nc.scalar.copy(out=b_bc[:], in_=rows_ps[0][:])
+        nc.scalar.copy(out=b2_bc[:], in_=rows_ps[1][:])
         quantise_w1(1)
+        cm1 = keep.tile([P, 4, NCODE], F32)
+        nc.vector.tensor_tensor(
+            out=cm1[:],
+            in0=smT[:, 0:4, 0:NCODE],
+            in1=smT[:, 0:4, ROW_B1 : ROW_B1 + 1].to_broadcast([P, 4, NCODE]),
+            op=ALU.add,
+        )
+        cms = keep.tile([P, NCODE], F32)
+        nc.vector.tensor_reduce(
+            out=cms[:], in_=cm1[:].rearrange("p t c -> p c t"), axis=AX.X, op=ALU.add
+        )
+        neg_g = keep.tile([P, 4], F32)
+        nc.gpsimd.tensor_scalar(
+            out=neg_g[:], in0=smT[:, 0:4, ROW_G], scalar1=-1.0, scalar2=0.0, op0=ALU.mult, op1=ALU.add
+        )
+        b_col = keep.tile([P, 4], F32)
+        nc.gpsimd.tensor_copy(out=b_col[:], in_=smT[:, 0:4, ROW_B])
+        w2g = keep.tile([P, CF, 4], BF16, align_bytes=64)
 
+        def g_copy(out, in_):
+            nc.gpsimd.tensor_scalar(out=out, in0=in_, scalar1=1.0, scalar2=0.0, op0=ALU.mult, op1=ALU.add)
+
+        for i in range(W2G):
+            regroup(g_copy, w2g[:, P * i : P * (i + 1)], w2_raw[:, :, P * i : P * (i + 1)])
+
+        dummy(D1)
         hpT_ps = [pso.tile([P, TOK], F32, tag="o", name="hpT_ps%d" % t) for t in range(4)]
         hp_ps = pso.tile([P, CF], F32, tag="o")
         for g in range(2):
+            nc.tensor.matmul_mx(
+                out=hp_ps[:],
+                lhsT=h_codes[:, TOK * g : TOK * (g + 1)].bitcast(FP8X4),
+                lhsT_scale=h_scales[:, TOK * g : TOK * (g + 1)],
+                rhs=w1_codes[:, g, :].bitcast(FP8X4),
+                rhs_scale=w1_scales[:, g, :],
+                start=(g == 0),
+                stop=(g == 1),
+            )
             for t in range(4):
                 nc.tensor.matmul_mx(
                     out=hpT_ps[t][:],
@@ -159,47 +215,11 @@ def tile_mixtureconfounderprior_pa_kernel(
                     start=(g == 0),
                     stop=(g == 1),
                 )
-            nc.tensor.matmul_mx(
-                out=hp_ps[:],
-                lhsT=h_codes[:, TOK * g : TOK * (g + 1)].bitcast(FP8X4),
-                lhsT_scale=h_scales[:, TOK * g : TOK * (g + 1)],
-                rhs=w1_codes[:, g, :].bitcast(FP8X4),
-                rhs_scale=w1_scales[:, g, :],
-                start=(g == 0),
-                stop=(g == 1),
-            )
-
-        smT = keep.tile([P, 6, 64], F32)
-        nc.scalar.copy(out=smT[:], in_=smT_ps[:, :, 0:64])
-        cm1 = keep.tile([P, 4, NCODE], F32)
-        nc.vector.tensor_tensor(
-            out=cm1[:],
-            in0=smT[:, 0:4, 0:NCODE],
-            in1=smT[:, 0:4, ROW_B1 : ROW_B1 + 1].to_broadcast([P, 4, NCODE]),
-            op=ALU.add,
-        )
-        neg_g = keep.tile([P, 4], F32)
-        nc.gpsimd.tensor_scalar(
-            out=neg_g[:], in0=smT[:, 0:4, ROW_G], scalar1=-1.0, scalar2=0.0, op0=ALU.mult, op1=ALU.add
-        )
-        b_col = keep.tile([P, 4], F32)
-        nc.gpsimd.tensor_copy(out=b_col[:], in_=smT[:, 0:4, ROW_B])
-        cms = keep.tile([P, NCODE], F32)
-        nc.vector.tensor_reduce(
-            out=cms[:], in_=cm1[:].rearrange("p t c -> p c t"), axis=AX.X, op=ALU.add
-        )
-        b_bc = keep.tile([P, CF], F32)
-        b2_bc = keep.tile([P, CF], F32)
-        nc.scalar.copy(out=b_bc[:], in_=rows_ps[0][:])
-        nc.scalar.copy(out=b2_bc[:], in_=rows_ps[1][:])
-        mc_ps = pso.tile([P, NCODE], F32, tag="o")
+            if g == 0:
+                mc_ps = psr.tile([P, NCODE], F32, tag="r")
         nc.tensor.matmul(mc_ps[:], lhsT=ones[:], rhs=cms[:], start=True, stop=True)
-        hpT_v = keep.tile([P, 2, TOK], F32)
-        hpT_s = keep.tile([P, 2, TOK], F32)
-        for i in range(2):
-            nc.vector.tensor_copy(out=hpT_v[:, i, :], in_=hpT_ps[i][:])
-            nc.scalar.copy(out=hpT_s[:, i, :], in_=hpT_ps[2 + i][:])
-        hpT = [hpT_v[:, 0, :], hpT_v[:, 1, :], hpT_s[:, 0, :], hpT_s[:, 1, :]]
+        st = keep.tile([P, 6], F32)
+        nc.vector.bn_stats(out=st[:], in_=hp_ps[:])
         c_sb = keep.tile([P, 4, NCODE], F32)
         nc.vector.tensor_tensor(
             out=c_sb[:],
@@ -207,17 +227,26 @@ def tile_mixtureconfounderprior_pa_kernel(
             in1=mc_ps[:].unsqueeze(1).to_broadcast([P, 4, NCODE]),
             op=ALU.subtract,
         )
+        hpT = keep.tile([P, 4, TOK], F32)
+        for t in range(4):
+            nc.scalar.copy(out=hpT[:, t, :], in_=hpT_ps[t][:])
+        for i in range(W2G, W2G + W2S):
+            regroup(nc.scalar.copy, w2g[:, P * i : P * (i + 1)], w2_raw[:, :, P * i : P * (i + 1)])
+        mv = keep.tile([P, 2], F32)
+        nc.vector.bn_aggr(out=mv[:], in_=st[:])
         csq = keep.tile([P, 4, NCODE], F32)
         nc.vector.tensor_tensor(out=csq[:], in0=c_sb[:], in1=c_sb[:], op=ALU.mult)
         cvs = keep.tile([P, NCODE], F32)
         nc.vector.tensor_reduce(
             out=cvs[:], in_=csq[:].rearrange("p t c -> p c t"), axis=AX.X, op=ALU.add
         )
+        vhe = keep.tile([P, 1], F32)
+        nc.vector.tensor_scalar_add(out=vhe[:], in0=mv[:, 1:2], scalar1=LN_EPS)
         hpTg = keep.tile([P, 4, TOK], F32)
         for t in range(4):
             nc.gpsimd.tensor_scalar(
                 out=hpTg[:, t, :],
-                in0=hpT[t],
+                in0=hpT[:, t, :],
                 scalar1=smT[:, t, ROW_G : ROW_G + 1],
                 scalar2=0.0,
                 op0=ALU.mult,
@@ -230,27 +259,21 @@ def tile_mixtureconfounderprior_pa_kernel(
             in1=smT[:, 0:4, ROW_G : ROW_G + 1].to_broadcast([P, 4, NCODE]),
             op=ALU.mult,
         )
-        w2g = keep.tile([P, CF, 4], BF16, align_bytes=64)
-        regroup(nc.scalar.copy, w2g[:, 0 : CF // 2], w2_raw[:, :, 0 : CF // 2])
 
-        v_ps = pso.tile([P, NCODE], F32, tag="o")
-        for t in range(4):
-            nc.tensor.matmul(v_ps[:], lhsT=hpT[t], rhs=c_sb[:, t, :], start=(t == 0), stop=False)
-        nc.tensor.matmul(v_ps[:], lhsT=halves[:], rhs=cvs[:], start=False, stop=True)
-        st = keep.tile([P, 6], F32)
-        nc.vector.bn_stats(out=st[:], in_=hp_ps[:])
-        mv = keep.tile([P, 2], F32)
-        nc.vector.bn_aggr(out=mv[:], in_=st[:])
-        vhe = keep.tile([P, 1], F32)
-        nc.vector.tensor_scalar_add(out=vhe[:], in0=mv[:, 1:2], scalar1=LN_EPS)
         mh_ps = pso.tile([P, TOK], F32, tag="o")
         nc.tensor.transpose(mh_ps[:], mv[:, 0:1].to_broadcast([P, P]), ident[:])
+        v_ps = pso.tile([P, NCODE], F32, tag="o")
+        for t in range(4):
+            nc.tensor.matmul(v_ps[:], lhsT=hpT[:, t, :], rhs=c_sb[:, t, :], start=(t == 0), stop=False)
+        nc.tensor.matmul(v_ps[:], lhsT=halves[:], rhs=cvs[:], start=False, stop=True)
+        dummy(D2)
         std = keep.tile([P, NCODE], F32)
         nc.scalar.activation(
             out=std[:], in_=v_ps[:], func=ACT.Sqrt, bias=vhe[:, 0:1], scale=2.0 / CF
         )
         nc.scalar.activation(out=warm[:], in_=eps[:], func=ACT.Tanh)
-        regroup(nc.scalar.copy, w2g[:, CF // 2 : CF], w2_raw[:, :, CF // 2 : CF])
+        for i in range(W2G + W2S, 4):
+            regroup(nc.scalar.copy, w2g[:, P * i : P * (i + 1)], w2_raw[:, :, P * i : P * (i + 1)])
         w2_codes = keep.tile([P, CF], U32, align_bytes=64)
         w2_scales = keep.tile([P, CF], U8, align_bytes=64)
         a_sb = keep.tile([P, 4, TOK], F32)
@@ -266,32 +289,38 @@ def tile_mixtureconfounderprior_pa_kernel(
         r_sb = keep.tile([P, NCODE], F32)
         nc.vector.reciprocal(out=r_sb[:], in_=std[:])
 
+        def quantise_w2():
+            nc.vector.quantize_mx(
+                out=w2_codes[:].bitcast(FP8X4),
+                scales=w2_scales[:],
+                in_=w2g[:].rearrange("p c t -> p (c t)"),
+            )
+
         tiles = {}
 
         def codes_of(rd, kinds):
-            return [cl for cl in range(CG) if KINDS[rd][cl] in kinds]
+            return [cl for cl in range(len(KINDS[rd])) if KINDS[rd][cl] in kinds]
 
         def bcast_r(rd):
             cls = codes_of(rd, "gv")
-            if rd > 0 and cls:
-                r_ps = psr.tile([P, CG, TOK], F32, tag="r", name="r_ps")
-                tiles[("rt", rd)] = r_ps
+            if not cls:
+                return
+            r_ps = psr.tile([P, 4, TOK], F32, tag="r", name="r_ps")
+            tiles[("rt", rd)] = r_ps
             for i, cl in enumerate(cls):
-                code = CG * rd + cl
-                if rd == 0:
-                    r_one = pso.tile([P, TOK], F32, tag="o", name="r_one")
-                    tiles[("r", rd, cl)] = r_one[:]
-                else:
-                    tiles[("r", rd, cl)] = tiles[("rt", rd)][:, i, :]
+                code = FIRST[rd] + cl
+                tiles[("r", rd, cl)] = r_ps[:, i, :]
                 nc.tensor.transpose(
-                    tiles[("r", rd, cl)], r_sb[:, code : code + 1].to_broadcast([P, P]), ident[:]
+                    r_ps[:, i, :], r_sb[:, code : code + 1].to_broadcast([P, P]), ident[:]
                 )
 
-        def normalise(rd):
-            z = work.tile([P, 4, CG, TOK], F32, name="z")
-            tiles[("z", rd)] = z
-            for cl in codes_of(rd, "gv"):
-                code = CG * rd + cl
+        def normalise(rd, cls):
+            if ("z", rd) not in tiles:
+                z = work.tile([P, 4, 4, TOK], F32, name="z")
+                tiles[("z", rd)] = z
+            z = tiles[("z", rd)]
+            for cl in cls:
+                code = FIRST[rd] + cl
                 for t in range(4):
                     nc.vector.scalar_tensor_tensor(
                         out=z[:, t, cl, :],
@@ -304,26 +333,25 @@ def tile_mixtureconfounderprior_pa_kernel(
 
         def mg_of(rd):
             if ("mg", rd) not in tiles:
-                mg = work.tile([P, W, 4], BF16, align_bytes=64, name="mg")
+                mg = work.tile([P, len(KINDS[rd]) * TOK, 4], BF16, align_bytes=64, name="mg")
                 tiles[("mg", rd)] = mg
             return tiles[("mg", rd)]
 
         def add_bias(rd, kind):
-            z = tiles[("z", rd)]
             engine = nc.gpsimd if kind == "g" else nc.vector
             for cl in codes_of(rd, kind):
                 engine.tensor_tensor(
                     out=mg_of(rd)[:, TOK * cl : TOK * (cl + 1), :].rearrange(
                         "p (c i) t -> p c t i", i=4
                     ),
-                    in0=z[:, :, cl, :].rearrange("p t (c i) -> p c t i", i=4),
+                    in0=tiles[("z", rd)][:, :, cl, :].rearrange("p t (c i) -> p c t i", i=4),
                     in1=b_col[:].unsqueeze(1).unsqueeze(3).to_broadcast([P, TOK // 4, 4, 4]),
                     op=ALU.add,
                 )
 
         def sum_rows(rd):
             for cl in codes_of(rd, "e"):
-                code = CG * rd + cl
+                code = FIRST[rd] + cl
                 u = pso.tile([P, 4, P], F32, tag="o", name="u")
                 tiles[("u", rd, cl)] = u
                 for t in range(4):
@@ -341,7 +369,7 @@ def tile_mixtureconfounderprior_pa_kernel(
 
         def scale_rows(rd):
             for cl in codes_of(rd, "e"):
-                code = CG * rd + cl
+                code = FIRST[rd] + cl
                 x = work.tile([P, CF], BF16, name="x")
                 tiles[("x", rd, cl)] = x
                 nc.vector.scalar_tensor_tensor(
@@ -355,6 +383,8 @@ def tile_mixtureconfounderprior_pa_kernel(
 
         def turn_rows(rd):
             cls = codes_of(rd, "e")
+            if not cls:
+                return
             xt_ps = pso.tile([P, len(cls), 2, TOK], F32, tag="o", name="xt_ps")
             tiles[("xt", rd)] = xt_ps
             for i, cl in enumerate(cls):
@@ -364,6 +394,8 @@ def tile_mixtureconfounderprior_pa_kernel(
 
         def copy_rows(rd):
             cls = codes_of(rd, "e")
+            if not cls:
+                return
             part = mg_of(rd)[:, TOK * cls[0] : TOK * (cls[-1] + 1), :].bitcast(F32)
             nc.scalar.copy(
                 out=part.rearrange("p (c r) u -> p c r u", r=TOK),
@@ -371,8 +403,9 @@ def tile_mixtureconfounderprior_pa_kernel(
             )
 
         def quantise_mu(rd):
-            mu_codes = work.tile([P, W], U32, align_bytes=64, name="mu_codes")
-            mu_scales = work.tile([P, W], U8, align_bytes=64, name="mu_scales")
+            w = len(KINDS[rd]) * TOK
+            mu_codes = work.tile([P, w], U32, align_bytes=64, name="mu_codes")
+            mu_scales = work.tile([P, w], U8, align_bytes=64, name="mu_scales")
             tiles[("q", rd)] = (mu_codes, mu_scales)
             nc.vector.quantize_mx(
                 out=mu_codes[:].bitcast(FP8X4),
@@ -380,26 +413,22 @@ def tile_mixtureconfounderprior_pa_kernel(
                 in_=mg_of(rd)[:].rearrange("p w t -> p (w t)"),
             )
 
-        def second_mm(rd):
+        def wide(rd):
+            return CF - P * KB[rd]
+
+        def a_groups(rd):
+            return range(0, len(KINDS[rd]), CF // wide(rd))
+
+        def blocks(rd):
+            return range(BLK - KB[rd], BLK)
+
+        def mm_a(rd):
             mu_codes, mu_scales = tiles[("q", rd)]
-            res = work.tile([P, CG, CF], F32, name="res")
-            tiles[("res", rd)] = res
-            kb = KB[rd]
-            wa = CF - P * kb
-            for nb in range(CF // P - kb, CF // P):
-                o_ps = pso.tile([P, W], F32, tag="o", name="ob_ps")
-                tiles[("ob", rd, nb)] = o_ps
-                nc.tensor.matmul_mx(
-                    out=o_ps[:],
-                    lhsT=w2_codes[:, P * nb : P * (nb + 1)].bitcast(FP8X4),
-                    lhsT_scale=w2_scales[:, P * nb : P * (nb + 1)],
-                    rhs=mu_codes[:].bitcast(FP8X4),
-                    rhs_scale=mu_scales[:],
-                    start=True,
-                    stop=True,
-                )
+            wa = wide(rd)
             per = CF // wa
-            for c0 in range(0, CG, per):
+            res = work.tile([P, len(KINDS[rd]), CF], F32, name="res")
+            tiles[("res", rd)] = res
+            for c0 in a_groups(rd):
                 o_ps = pso.tile([P, per, wa], F32, tag="o", name="oa_ps")
                 tiles[("oa", rd, c0)] = o_ps
                 for i in range(per):
@@ -414,9 +443,24 @@ def tile_mixtureconfounderprior_pa_kernel(
                         stop=True,
                     )
 
+        def mm_b(rd):
+            mu_codes, mu_scales = tiles[("q", rd)]
+            for nb in blocks(rd):
+                o_ps = pso.tile([P, len(KINDS[rd]) * TOK], F32, tag="o", name="ob_ps")
+                tiles[("ob", rd, nb)] = o_ps
+                nc.tensor.matmul_mx(
+                    out=o_ps[:],
+                    lhsT=w2_codes[:, P * nb : P * (nb + 1)].bitcast(FP8X4),
+                    lhsT_scale=w2_scales[:, P * nb : P * (nb + 1)],
+                    rhs=mu_codes[:].bitcast(FP8X4),
+                    rhs_scale=mu_scales[:],
+                    start=True,
+                    stop=True,
+                )
+
         def tanh_b(rd):
-            for nb in range(CF // P - KB[rd], CF // P):
-                th = work.tile([P, W], F32, name="th")
+            for nb in blocks(rd):
+                th = work.tile([P, len(KINDS[rd]) * TOK], F32, name="th")
                 tiles[("th", rd, nb)] = th
                 nc.scalar.activation(
                     out=th[:],
@@ -426,81 +470,67 @@ def tile_mixtureconfounderprior_pa_kernel(
                 )
 
         def turn_b(rd):
-            for nb in range(CF // P - KB[rd], CF // P):
-                tr = pso.tile([P, CG, P], F32, tag="o", name="tr")
+            for nb in blocks(rd):
+                tr = pso.tile([P, len(KINDS[rd]), P], F32, tag="o", name="tr")
                 tiles[("tr", rd, nb)] = tr
-                for cl in range(CG):
+                for cl in range(len(KINDS[rd])):
                     nc.tensor.transpose(
                         tr[:, cl, :], tiles[("th", rd, nb)][:, TOK * cl : TOK * (cl + 1)], ident[:]
                     )
 
         def copy_b(rd):
-            for nb in range(CF // P - KB[rd], CF // P):
+            for nb in blocks(rd):
                 nc.scalar.copy(
                     out=tiles[("res", rd)][:, :, P * nb : P * (nb + 1)], in_=tiles[("tr", rd, nb)][:]
                 )
 
         def add_a(rd, c0, lo=0, hi=CF):
-            o_ps = tiles[("oa", rd, c0)]
-            wa = CF - P * KB[rd]
+            wa = wide(rd)
             hi = min(hi, wa)
             per = CF // wa
             nc.vector.tensor_tensor(
                 out=tiles[("res", rd)][:, c0 : c0 + per, lo:hi],
-                in0=o_ps[:, :, lo:hi],
+                in0=tiles[("oa", rd, c0)][:, :, lo:hi],
                 in1=b2_bc[:, lo:hi].unsqueeze(1).to_broadcast([P, per, hi - lo]),
                 op=ALU.add,
             )
 
         def tanh_a(rd, c0, lo=0, hi=CF):
-            wa = CF - P * KB[rd]
-            hi = min(hi, wa)
-            part = tiles[("res", rd)][:, c0 : c0 + CF // wa, lo:hi]
+            hi = min(hi, wide(rd))
+            part = tiles[("res", rd)][:, c0 : c0 + CF // wide(rd), lo:hi]
             nc.scalar.activation(out=part, in_=part, func=ACT.Tanh)
 
         def store(rd, c0, c1, lo=0, hi=CF):
             nc.sync.dma_start(
-                out=out3[:, CG * rd + c0 : CG * rd + c1, lo:hi],
+                out=out3[:, FIRST[rd] + c0 : FIRST[rd] + c1, lo:hi],
                 in_=tiles[("res", rd)][:, c0:c1, lo:hi],
             )
 
-        def a_groups(rd):
-            return range(0, CG, CF // (CF - P * KB[rd]))
-
+        last = ROUNDS - 1
         bcast_r(0)
-        sum_rows(0)
-        normalise(0)
-        add_bias(0, "g")
-        scale_rows(0)
-        add_bias(0, "v")
         bcast_r(1)
-        turn_rows(0)
-        copy_rows(0)
         sum_rows(1)
-        nc.vector.quantize_mx(
-            out=w2_codes[:].bitcast(FP8X4),
-            scales=w2_scales[:],
-            in_=w2g[:].rearrange("p c t -> p (c t)"),
-        )
+        dummy(DA)
+        normalise(0, codes_of(0, "gv"))
+        add_bias(0, "g")
+        quantise_w2()
+        add_bias(0, "v")
         scale_rows(1)
         turn_rows(1)
-        last = ROUNDS - 1
-        for rd in range(ROUNDS):
+        for rd in range(last):
             quantise_mu(rd)
-            second_mm(rd)
+            mm_a(rd)
+            mm_b(rd)
             if rd + 2 < ROUNDS:
                 bcast_r(rd + 2)
                 sum_rows(rd + 2)
-            if rd + 1 < ROUNDS:
-                normalise(rd + 1)
-                add_bias(rd + 1, "g")
+                dummy(DC if rd else DB)
+            normalise(rd + 1, codes_of(rd + 1, "gv"))
+            add_bias(rd + 1, "g")
             if rd > 0:
                 copy_b(rd - 1)
-                store(rd - 1, 0, CG)
-            if rd + 1 < ROUNDS:
-                copy_rows(rd + 1)
-            if rd == last:
-                break
+                store(rd - 1, 0, len(KINDS[rd - 1]))
+            copy_rows(rd + 1)
             tanh_b(rd)
             turn_b(rd)
             for c0 in a_groups(rd):
@@ -511,13 +541,16 @@ def tile_mixtureconfounderprior_pa_kernel(
             if rd + 2 < ROUNDS:
                 scale_rows(rd + 2)
                 turn_rows(rd + 2)
-        for c0 in range(CG - 1):
+        quantise_mu(last)
+        mm_a(last)
+        copy_b(last - 1)
+        store(last - 1, 0, len(KINDS[last - 1]))
+        n = len(KINDS[last])
+        for c0 in range(n - 1):
             add_a(last, c0)
-        for c0 in range(CG - 1):
             tanh_a(last, c0)
-            if c0 > 0:
-                store(last, 0 if c0 == 1 else c0, c0 + 1)
+            store(last, c0, c0 + 1)
         for lo in (0, CF // 2):
-            add_a(last, CG - 1, lo, lo + CF // 2)
-            tanh_a(last, CG - 1, lo, lo + CF // 2)
-            store(last, CG - 1, CG, lo, lo + CF // 2)
+            add_a(last, n - 1, lo, lo + CF // 2)
+            tanh_a(last, n - 1, lo, lo + CF // 2)
+            store(last, n - 1, n, lo, lo + CF // 2)

@@ -28,16 +28,17 @@ ROW_B2 = 56
 W1_V = 288
 W1_V2 = 288
 D0 = 3
-D1 = 3
+D1 = 0
 D2 = 2
 DA = 4
 DB = 4
 DC = 2
 W2G = 2
 W2S = 2
+Q0FIRST = 0
 
 
-KINDS = ["gv","ggee","ggee","ggee","ggee","ggee","ggee","ggee","gv"]
+KINDS = ["vv","ggee","ggee","ggee","ggee","ggee","ggee","gvee","vv"]
 KB = [0,2,2,2,2,2,2,0,0]
 FIRST = [sum(len(k) for k in KINDS[:i]) for i in range(len(KINDS))]
 ROUNDS = len(KINDS)
@@ -104,6 +105,8 @@ def tile_mixtureconfounderprior_pa_kernel(
         nc.scalar.activation(out=warm[:], in_=eps[:], func=ACT.Sqrt)
 
         def dummy(n):
+            if n == 0:
+                return
             busy = pso.tile([P, P], F32, tag="o", name="busy")
             for i in range(n):
                 nc.tensor.matmul(busy[:], lhsT=ident[:], rhs=ident[:], start=True, stop=True)
@@ -164,7 +167,10 @@ def tile_mixtureconfounderprior_pa_kernel(
         nc.scalar.copy(out=smT[:], in_=smT_ps[:, :, 0:64])
         b_bc = keep.tile([P, CF], F32)
         b2_bc = keep.tile([P, CF], F32)
-        nc.scalar.copy(out=b_bc[:], in_=rows_ps[0][:])
+        nc.scalar.copy(
+            out=b_bc[:].rearrange("q (u p e) -> q u p e", u=2, e=2),
+            in_=rows_ps[0][:].rearrange("q (p u e) -> q u p e", u=2, e=2),
+        )
         nc.scalar.copy(out=b2_bc[:], in_=rows_ps[1][:])
         quantise_w1(1)
         cm1 = keep.tile([P, 4, NCODE], F32)
@@ -331,6 +337,9 @@ def tile_mixtureconfounderprior_pa_kernel(
                         op1=ALU.mult,
                     )
 
+        def token():
+            nc.vector.tensor_copy(out=b_col[:], in_=smT[:, 0:4, ROW_B])
+
         def mg_of(rd):
             if ("mg", rd) not in tiles:
                 mg = work.tile([P, len(KINDS[rd]) * TOK, 4], BF16, align_bytes=64, name="mg")
@@ -372,14 +381,16 @@ def tile_mixtureconfounderprior_pa_kernel(
                 code = FIRST[rd] + cl
                 x = work.tile([P, CF], BF16, name="x")
                 tiles[("x", rd, cl)] = x
-                nc.vector.scalar_tensor_tensor(
-                    out=x[:].rearrange("p (r t) -> p r t", t=4),
-                    in0=tiles[("u", rd, cl)][:].rearrange("p t r -> p r t"),
-                    scalar=r_sb[:, code : code + 1],
-                    in1=b_bc[:].rearrange("p (r t) -> p r t", t=4),
-                    op0=ALU.mult,
-                    op1=ALU.add,
-                )
+                for u in range(2):
+                    half = slice(2 * P * u, 2 * P * (u + 1))
+                    nc.vector.scalar_tensor_tensor(
+                        out=x[:, half].rearrange("p (r e) -> p r e", e=2),
+                        in0=tiles[("u", rd, cl)][:, 2 * u : 2 * u + 2, :].rearrange("p e r -> p r e"),
+                        scalar=r_sb[:, code : code + 1],
+                        in1=b_bc[:, half].rearrange("p (r e) -> p r e", e=2),
+                        op0=ALU.mult,
+                        op1=ALU.add,
+                    )
 
         def turn_rows(rd):
             cls = codes_of(rd, "e")
@@ -390,7 +401,7 @@ def tile_mixtureconfounderprior_pa_kernel(
             for i, cl in enumerate(cls):
                 words = tiles[("x", rd, cl)][:].bitcast(F32)
                 for u in range(2):
-                    nc.tensor.transpose(xt_ps[:, i, u, :], words[:, u : CF // 2 : 2], ident[:])
+                    nc.tensor.transpose(xt_ps[:, i, u, :], words[:, P * u : P * (u + 1)], ident[:])
 
         def copy_rows(rd):
             cls = codes_of(rd, "e")
@@ -511,40 +522,64 @@ def tile_mixtureconfounderprior_pa_kernel(
         bcast_r(1)
         sum_rows(1)
         dummy(DA)
+        quantise_w2()
         normalise(0, codes_of(0, "gv"))
         add_bias(0, "g")
-        quantise_w2()
         add_bias(0, "v")
-        scale_rows(1)
-        turn_rows(1)
+        if Q0FIRST == 0:
+            scale_rows(1)
+            turn_rows(1)
         for rd in range(last):
             quantise_mu(rd)
+            token()
             mm_a(rd)
             mm_b(rd)
-            if rd + 2 < ROUNDS:
-                bcast_r(rd + 2)
-                sum_rows(rd + 2)
-                dummy(DC if rd else DB)
-            normalise(rd + 1, codes_of(rd + 1, "gv"))
+            if rd == 0:
+                bcast_r(2)
+                sum_rows(2)
+                dummy(DB)
+                normalise(1, codes_of(1, "gv"))
+                if Q0FIRST:
+                    scale_rows(1)
+                    turn_rows(1)
+            else:
+                if rd + 2 < ROUNDS:
+                    sum_rows(rd + 2)
+                    dummy(DC)
             add_bias(rd + 1, "g")
             if rd > 0:
                 copy_b(rd - 1)
-                store(rd - 1, 0, len(KINDS[rd - 1]))
+                if KB[rd - 1]:
+                    store(rd - 1, 0, len(KINDS[rd - 1]))
             copy_rows(rd + 1)
             tanh_b(rd)
             turn_b(rd)
-            for c0 in a_groups(rd):
-                add_a(rd, c0)
+            if rd == 0:
+                for c0 in a_groups(rd):
+                    add_a(rd, c0)
+            if rd + 2 < ROUNDS:
+                normalise(rd + 2, codes_of(rd + 2, "gv"))
+            if rd == last - 1:
+                add_bias(last, "v")
+                quantise_mu(last)
+                mm_a(last)
+            if rd > 0:
+                for c0 in a_groups(rd):
+                    add_a(rd, c0)
             for c0 in a_groups(rd):
                 tanh_a(rd, c0)
-            add_bias(rd + 1, "v")
+                if KB[rd] == 0:
+                    store(rd, c0, c0 + 1)
+            if rd < last - 1:
+                add_bias(rd + 1, "v")
+            if rd + 3 < ROUNDS:
+                bcast_r(rd + 3)
             if rd + 2 < ROUNDS:
                 scale_rows(rd + 2)
                 turn_rows(rd + 2)
-        quantise_mu(last)
-        mm_a(last)
         copy_b(last - 1)
-        store(last - 1, 0, len(KINDS[last - 1]))
+        if KB[last - 1]:
+            store(last - 1, 0, len(KINDS[last - 1]))
         n = len(KINDS[last])
         for c0 in range(n - 1):
             add_a(last, c0)

@@ -350,11 +350,9 @@ def tile_mixtureconfounderprior_pa_kernel(
             engine = nc.gpsimd if kind == "g" else nc.vector
             for cl in codes_of(rd, kind):
                 engine.tensor_tensor(
-                    out=mg_of(rd)[:, TOK * cl : TOK * (cl + 1), :].rearrange(
-                        "p (c i) t -> p c t i", i=4
-                    ),
-                    in0=tiles[("z", rd)][:, :, cl, :].rearrange("p t (c i) -> p c t i", i=4),
-                    in1=b_col[:].unsqueeze(1).unsqueeze(3).to_broadcast([P, TOK // 4, 4, 4]),
+                    out=mg_of(rd)[:, TOK * cl : TOK * (cl + 1), :],
+                    in0=tiles[("z", rd)][:, :, cl, :].rearrange("p t r -> p r t"),
+                    in1=b_col[:].unsqueeze(1).to_broadcast([P, TOK, 4]),
                     op=ALU.add,
                 )
 

@@ -95,6 +95,11 @@ def tile_mixtureconfounderprior_pa_kernel(
         make_identity(nc, ident[:])
         ident_bf = keep.tile([P, P], BF16)
         make_identity(nc, ident_bf[:])
+        first = keep.tile([P, 4], BF16)
+        nc.gpsimd.tensor_tensor(out=first[:], in0=ident[:, 0:4], in1=ident[:, 4:8], op=ALU.add)
+        nc.gpsimd.tensor_scalar(
+            out=first[:], in0=ident[:, 0:4], scalar1=ident[:, 4:5], scalar2=0.0, op0=ALU.mult, op1=ALU.add
+        )
         ones = keep.tile([P, P], F32)
         nc.vector.memset(ones[:], 1.0 / CF)
         halves = keep.tile([P, P], F32)
@@ -189,7 +194,9 @@ def tile_mixtureconfounderprior_pa_kernel(
             out=neg_g[:], in0=smT[:, 0:4, ROW_G], scalar1=-1.0, scalar2=0.0, op0=ALU.mult, op1=ALU.add
         )
         b_col = keep.tile([P, 4], F32)
-        nc.gpsimd.tensor_copy(out=b_col[:], in_=smT[:, 0:4, ROW_B])
+        nc.gpsimd.tensor_scalar(
+            out=b_col[:], in0=smT[:, 0:4, ROW_B], scalar1=1.0, scalar2=0.0, op0=ALU.mult, op1=ALU.add
+        )
         w2g = keep.tile([P, CF, 4], BF16, align_bytes=64)
 
         def g_copy(out, in_):
@@ -259,7 +266,7 @@ def tile_mixtureconfounderprior_pa_kernel(
                 op1=ALU.add,
             )
         cg = keep.tile([P, 4, NCODE], F32)
-        nc.gpsimd.tensor_tensor(
+        nc.vector.tensor_tensor(
             out=cg[:],
             in0=c_sb[:],
             in1=smT[:, 0:4, ROW_G : ROW_G + 1].to_broadcast([P, 4, NCODE]),

@@ -29,16 +29,24 @@ W1_V = 288
 W1_V2 = 288
 D0 = 3
 D1 = 0
-D2 = 2
+D2 = 0
 DA = 4
-DB = 4
+DB = 3
 DC = 2
 W2G = 2
 W2S = 2
+CBF = 0
+BNFIRST = 0
+TAIL = 0
+G8 = 0
+SPLIT = 6
+D3 = 3
+HALF1 = 1
+SPOS = 1
 Q0FIRST = 0
 
 
-KINDS = ["vv","ggee","ggee","ggee","ggee","ggee","ggee","gvee","vv"]
+KINDS = ["SS","ggee","ggee","ggee","ggee","ggee","ggee","gvee","vv"]
 KB = [0,2,2,2,2,2,2,0,0]
 FIRST = [sum(len(k) for k in KINDS[:i]) for i in range(len(KINDS))]
 ROUNDS = len(KINDS)
@@ -89,17 +97,12 @@ def tile_mixtureconfounderprior_pa_kernel(
         nc.scalar.dma_start(out=sm_raw[ROW_B2 : ROW_B2 + 8, :], in_=mu_b2.partition_broadcast(8))
         nc.vector.memset(sm_raw[64:128, :].bitcast(F32), 0.0)
         w2_raw = keep.tile([P, 4, CF], BF16)
-        nc.scalar.dma_start(out=w2_raw[:], in_=mu_w2.rearrange("(p t) n -> p t n", t=4))
+        nc.sync.dma_start(out=w2_raw[:], in_=mu_w2.rearrange("(p t) n -> p t n", t=4))
 
         ident = keep.tile([P, P], F32)
         make_identity(nc, ident[:])
         ident_bf = keep.tile([P, P], BF16)
         make_identity(nc, ident_bf[:])
-        first = keep.tile([P, 4], BF16)
-        nc.gpsimd.tensor_tensor(out=first[:], in0=ident[:, 0:4], in1=ident[:, 4:8], op=ALU.add)
-        nc.gpsimd.tensor_scalar(
-            out=first[:], in0=ident[:, 0:4], scalar1=ident[:, 4:5], scalar2=0.0, op0=ALU.mult, op1=ALU.add
-        )
         ones = keep.tile([P, P], F32)
         nc.vector.memset(ones[:], 1.0 / CF)
         halves = keep.tile([P, P], F32)
@@ -107,7 +110,7 @@ def tile_mixtureconfounderprior_pa_kernel(
         eps = keep.tile([P, 1], F32)
         nc.vector.memset(eps[:], LN_EPS)
         warm = keep.tile([P, 1], F32)
-        nc.scalar.activation(out=warm[:], in_=eps[:], func=ACT.Sqrt)
+        nc.scalar.activation(out=warm[:], in_=eps[:], func=ACT.Abs_reciprocal_sqrt)
 
         def dummy(n):
             if n == 0:
@@ -160,14 +163,15 @@ def tile_mixtureconfounderprior_pa_kernel(
 
         regroup_w1(nc.vector.tensor_copy, w1g[:, 0], w1_raw[:, 0], 0, W1_V // 4)
         regroup_w1(nc.scalar.copy, w1g[:, 0], w1_raw[:, 0], W1_V // 4, P)
+        regroup_w1(nc.vector.tensor_copy, w1g[:, 1], w1_raw[:, 1], 0, W1_V2 // 4)
+        regroup_w1(nc.scalar.copy, w1g[:, 1], w1_raw[:, 1], W1_V2 // 4, P)
         nc.vector.quantize_mx(
             out=h_codes[:].bitcast(FP8X4),
             scales=h_scales[:],
             in_=hg[:].rearrange("p g r t -> p (g r t)"),
         )
         quantise_w1(0)
-        regroup_w1(nc.vector.tensor_copy, w1g[:, 1], w1_raw[:, 1], 0, W1_V2 // 4)
-        regroup_w1(nc.scalar.copy, w1g[:, 1], w1_raw[:, 1], W1_V2 // 4, P)
+        quantise_w1(1)
         smT = keep.tile([P, 6, 64], F32)
         nc.scalar.copy(out=smT[:], in_=smT_ps[:, :, 0:64])
         b_bc = keep.tile([P, CF], F32)
@@ -177,7 +181,6 @@ def tile_mixtureconfounderprior_pa_kernel(
             in_=rows_ps[0][:].rearrange("q (p u e) -> q u p e", u=2, e=2),
         )
         nc.scalar.copy(out=b2_bc[:], in_=rows_ps[1][:])
-        quantise_w1(1)
         cm1 = keep.tile([P, 4, NCODE], F32)
         nc.vector.tensor_tensor(
             out=cm1[:],
@@ -190,20 +193,15 @@ def tile_mixtureconfounderprior_pa_kernel(
             out=cms[:], in_=cm1[:].rearrange("p t c -> p c t"), axis=AX.X, op=ALU.add
         )
         neg_g = keep.tile([P, 4], F32)
-        nc.gpsimd.tensor_scalar(
-            out=neg_g[:], in0=smT[:, 0:4, ROW_G], scalar1=-1.0, scalar2=0.0, op0=ALU.mult, op1=ALU.add
-        )
+        nc.vector.tensor_scalar_mul(out=neg_g[:], in0=smT[:, 0:4, ROW_G], scalar1=-1.0)
         b_col = keep.tile([P, 4], F32)
-        nc.gpsimd.tensor_scalar(
-            out=b_col[:], in0=smT[:, 0:4, ROW_B], scalar1=1.0, scalar2=0.0, op0=ALU.mult, op1=ALU.add
-        )
+        nc.vector.tensor_copy(out=b_col[:], in_=smT[:, 0:4, ROW_B])
         w2g = keep.tile([P, CF, 4], BF16, align_bytes=64)
 
-        def g_copy(out, in_):
-            nc.gpsimd.tensor_scalar(out=out, in0=in_, scalar1=1.0, scalar2=0.0, op0=ALU.mult, op1=ALU.add)
+        def regroup_w2(op, i):
+            regroup(op, w2g[:, P * i : P * (i + 1)], w2_raw[:, :, P * i : P * (i + 1)])
 
-        for i in range(W2G):
-            regroup(g_copy, w2g[:, P * i : P * (i + 1)], w2_raw[:, :, P * i : P * (i + 1)])
+        regroup_w2(nc.vector.tensor_copy, 0)
 
         dummy(D1)
         hpT_ps = [pso.tile([P, TOK], F32, tag="o", name="hpT_ps%d" % t) for t in range(4)]
@@ -231,9 +229,12 @@ def tile_mixtureconfounderprior_pa_kernel(
             if g == 0:
                 mc_ps = psr.tile([P, NCODE], F32, tag="r")
         nc.tensor.matmul(mc_ps[:], lhsT=ones[:], rhs=cms[:], start=True, stop=True)
+        dummy(D3)
+        c_sb = keep.tile([P, 4, NCODE], F32)
         st = keep.tile([P, 6], F32)
         nc.vector.bn_stats(out=st[:], in_=hp_ps[:])
-        c_sb = keep.tile([P, 4, NCODE], F32)
+        mv = keep.tile([P, 2], F32)
+        nc.vector.bn_aggr(out=mv[:], in_=st[:])
         nc.vector.tensor_tensor(
             out=c_sb[:],
             in0=cm1[:],
@@ -243,10 +244,12 @@ def tile_mixtureconfounderprior_pa_kernel(
         hpT = keep.tile([P, 4, TOK], F32)
         for t in range(4):
             nc.scalar.copy(out=hpT[:, t, :], in_=hpT_ps[t][:])
-        for i in range(W2G, W2G + W2S):
-            regroup(nc.scalar.copy, w2g[:, P * i : P * (i + 1)], w2_raw[:, :, P * i : P * (i + 1)])
-        mv = keep.tile([P, 2], F32)
-        nc.vector.bn_aggr(out=mv[:], in_=st[:])
+        hpTg = keep.tile([P, 4, TOK], F32)
+        for t in range(4):
+            nc.scalar.activation(
+                out=hpTg[:, t, :], in_=hpT_ps[t][:], func=ACT.Copy, scale=smT[:, t, ROW_G : ROW_G + 1]
+            )
+        regroup_w2(nc.scalar.copy, 1)
         csq = keep.tile([P, 4, NCODE], F32)
         nc.vector.tensor_tensor(out=csq[:], in0=c_sb[:], in1=c_sb[:], op=ALU.mult)
         cvs = keep.tile([P, NCODE], F32)
@@ -255,16 +258,6 @@ def tile_mixtureconfounderprior_pa_kernel(
         )
         vhe = keep.tile([P, 1], F32)
         nc.vector.tensor_scalar_add(out=vhe[:], in0=mv[:, 1:2], scalar1=LN_EPS)
-        hpTg = keep.tile([P, 4, TOK], F32)
-        for t in range(4):
-            nc.gpsimd.tensor_scalar(
-                out=hpTg[:, t, :],
-                in0=hpT[:, t, :],
-                scalar1=smT[:, t, ROW_G : ROW_G + 1],
-                scalar2=0.0,
-                op0=ALU.mult,
-                op1=ALU.add,
-            )
         cg = keep.tile([P, 4, NCODE], F32)
         nc.vector.tensor_tensor(
             out=cg[:],
@@ -280,13 +273,11 @@ def tile_mixtureconfounderprior_pa_kernel(
             nc.tensor.matmul(v_ps[:], lhsT=hpT[:, t, :], rhs=c_sb[:, t, :], start=(t == 0), stop=False)
         nc.tensor.matmul(v_ps[:], lhsT=halves[:], rhs=cvs[:], start=False, stop=True)
         dummy(D2)
-        std = keep.tile([P, NCODE], F32)
+        r_sb = keep.tile([P, NCODE], F32)
         nc.scalar.activation(
-            out=std[:], in_=v_ps[:], func=ACT.Sqrt, bias=vhe[:, 0:1], scale=2.0 / CF
+            out=r_sb[:], in_=v_ps[:], func=ACT.Abs_reciprocal_sqrt, bias=vhe[:, 0:1], scale=2.0 / CF
         )
         nc.scalar.activation(out=warm[:], in_=eps[:], func=ACT.Tanh)
-        for i in range(W2G + W2S, 4):
-            regroup(nc.scalar.copy, w2g[:, P * i : P * (i + 1)], w2_raw[:, :, P * i : P * (i + 1)])
         w2_codes = keep.tile([P, CF], U32, align_bytes=64)
         w2_scales = keep.tile([P, CF], U8, align_bytes=64)
         a_sb = keep.tile([P, 4, TOK], F32)
@@ -299,8 +290,9 @@ def tile_mixtureconfounderprior_pa_kernel(
                 op0=ALU.mult,
                 op1=ALU.add,
             )
-        r_sb = keep.tile([P, NCODE], F32)
-        nc.vector.reciprocal(out=r_sb[:], in_=std[:])
+
+        regroup_w2(nc.vector.tensor_copy, 2)
+        regroup_w2(nc.vector.tensor_copy, 3)
 
         def quantise_w2():
             nc.vector.quantize_mx(
@@ -315,7 +307,7 @@ def tile_mixtureconfounderprior_pa_kernel(
             return [cl for cl in range(len(KINDS[rd])) if KINDS[rd][cl] in kinds]
 
         def bcast_r(rd):
-            cls = codes_of(rd, "gv")
+            cls = codes_of(rd, "gvS")
             if not cls:
                 return
             r_ps = psr.tile([P, 4, TOK], F32, tag="r", name="r_ps")
@@ -353,15 +345,33 @@ def tile_mixtureconfounderprior_pa_kernel(
                 tiles[("mg", rd)] = mg
             return tiles[("mg", rd)]
 
-        def add_bias(rd, kind):
+        def add_bias(rd, kind, cls=None):
             engine = nc.gpsimd if kind == "g" else nc.vector
-            for cl in codes_of(rd, kind):
+            for cl in codes_of(rd, kind) if cls is None else cls:
                 engine.tensor_tensor(
                     out=mg_of(rd)[:, TOK * cl : TOK * (cl + 1), :],
                     in0=tiles[("z", rd)][:, :, cl, :].rearrange("p t r -> p r t"),
                     in1=b_col[:].unsqueeze(1).to_broadcast([P, TOK, 4]),
                     op=ALU.add,
                 )
+
+        def bias_planes(rd):
+            cls = codes_of(rd, "S")
+            if not cls:
+                return
+            m = work.tile([P, 4, len(cls), TOK], BF16, name="m")
+            for t in range(4):
+                nc.scalar.activation(
+                    out=m[:, t],
+                    in_=tiles[("z", rd)][:, t, cls[0] : cls[-1] + 1, :],
+                    func=ACT.Identity,
+                    bias=b_col[:, t : t + 1],
+                )
+            regroup(
+                nc.scalar.copy,
+                mg_of(rd)[:, TOK * cls[0] : TOK * (cls[-1] + 1), :],
+                m[:].rearrange("p t c r -> p t (c r)"),
+            )
 
         def sum_rows(rd):
             for cl in codes_of(rd, "e"):
@@ -527,13 +537,14 @@ def tile_mixtureconfounderprior_pa_kernel(
         bcast_r(1)
         sum_rows(1)
         dummy(DA)
-        quantise_w2()
-        normalise(0, codes_of(0, "gv"))
+        normalise(0, codes_of(0, "gvS"))
         add_bias(0, "g")
         add_bias(0, "v")
-        if Q0FIRST == 0:
-            scale_rows(1)
-            turn_rows(1)
+        bias_planes(0)
+        scale_rows(1)
+        turn_rows(1)
+        quantise_w2()
+        normalise(1, codes_of(1, "gvS")[:HALF1])
         for rd in range(last):
             quantise_mu(rd)
             token()
@@ -543,19 +554,23 @@ def tile_mixtureconfounderprior_pa_kernel(
                 bcast_r(2)
                 sum_rows(2)
                 dummy(DB)
-                normalise(1, codes_of(1, "gv"))
-                if Q0FIRST:
-                    scale_rows(1)
-                    turn_rows(1)
+                normalise(1, codes_of(1, "gvS")[HALF1:])
             else:
                 if rd + 2 < ROUNDS:
                     sum_rows(rd + 2)
                     dummy(DC)
-            add_bias(rd + 1, "g")
+            if rd < last - 1 or not G8:
+                add_bias(rd + 1, "g")
+            else:
+                add_bias(last, "g", codes_of(last, "g")[1:])
+            if rd == last - 2 and G8:
+                late_g = True
+            else:
+                late_g = False
             if rd > 0:
                 copy_b(rd - 1)
                 if KB[rd - 1]:
-                    store(rd - 1, 0, len(KINDS[rd - 1]))
+                    store(rd - 1, 0, len(KINDS[rd - 1]), wide(rd - 1) if rd - 1 >= SPLIT else 0)
             copy_rows(rd + 1)
             tanh_b(rd)
             turn_b(rd)
@@ -563,18 +578,28 @@ def tile_mixtureconfounderprior_pa_kernel(
                 for c0 in a_groups(rd):
                     add_a(rd, c0)
             if rd + 2 < ROUNDS:
-                normalise(rd + 2, codes_of(rd + 2, "gv"))
+                normalise(rd + 2, codes_of(rd + 2, "gvS"))
+            if late_g:
+                add_bias(last, "g", codes_of(last, "g")[:1])
+            groups = list(a_groups(rd))
+            ahead = 0
             if rd == last - 1:
+                ahead = TAIL
+                bias_planes(last)
                 add_bias(last, "v")
+                for c0 in groups[:ahead]:
+                    add_a(rd, c0)
                 quantise_mu(last)
                 mm_a(last)
             if rd > 0:
-                for c0 in a_groups(rd):
+                for c0 in groups[ahead:]:
                     add_a(rd, c0)
             for c0 in a_groups(rd):
                 tanh_a(rd, c0)
                 if KB[rd] == 0:
                     store(rd, c0, c0 + 1)
+                elif rd >= SPLIT:
+                    store(rd, c0, c0 + CF // wide(rd), 0, wide(rd))
             if rd < last - 1:
                 add_bias(rd + 1, "v")
             if rd + 3 < ROUNDS:

from contextlib import ExitStack

from concourse import mybir
from concourse.masks import make_identity

F32 = mybir.dt.float32
BF16 = mybir.dt.bfloat16
U32 = mybir.dt.uint32
U8 = mybir.dt.uint8
FP8X4 = mybir.dt.float8_e4m3fn_x4
ALU = mybir.AluOpType
ACT = mybir.ActivationFunctionType
AX = mybir.AxisListType

P = 128
TOK = 128
D_IN = 1024
CF = 512
NCODE = 32
LN_EPS = 1e-5

FLOPS = 2 * TOK * D_IN * CF + 2 * TOK * NCODE * CF * CF

ROW_B1 = 32
ROW_G = 40
ROW_B = 48
ROW_B2 = 56
W1_V = 288
W1_V2 = 288
D0 = 3
D1 = 0
D2 = 0
DA = 4
DB = 3
DC = 2
W2G = 2
W2S = 2
CBF = 0
BNFIRST = 0
TAIL = 0
G8 = 0
SPLIT = 6
D3 = 3
HALF1 = 1
SPOS = 1
Q0FIRST = 0


KINDS = ["SS","ggee","ggee","ggee","ggee","ggee","ggee","gvee","vv"]
KB = [0,2,2,2,2,2,2,0,0]
FIRST = [sum(len(k) for k in KINDS[:i]) for i in range(len(KINDS))]
ROUNDS = len(KINDS)
BLK = 4


def regroup(op, dst, src):
    op(
        out=dst.rearrange("p (c i) t -> p c t i", i=4),
        in_=src.rearrange("p t (c i) -> p c t i", i=4),
    )


def regroup_w1(op, dst, src, m0, m1):
    op(
        out=dst.rearrange("p (t m) j -> p t m j", t=4)[:, :, m0:m1],
        in_=src.rearrange("p j (m t) -> p t m j", t=4)[:, :, m0:m1],
    )


def tile_mixtureconfounderprior_pa_kernel(
    tc, h, mu_w1_h, code_mu, mu_b1, ln_g, ln_b, mu_w2, mu_b2, out
):
    nc = tc.nc
    h2 = h.rearrange("b t d -> (b t) d")
    out3 = out.rearrange("b t k n -> (b t) k n")

    with ExitStack() as ctx:
        keep = ctx.enter_context(tc.tile_pool(name="keep", bufs=1))
        work = ctx.enter_context(tc.tile_pool(name="work", bufs=3))
        psr = ctx.enter_context(tc.psum_pool(name="psr", bufs=2))
        pso = ctx.enter_context(tc.psum_pool(name="pso", bufs=6))
        ctx.enter_context(tc.manual_schedule())

        h_sb = keep.tile([P, D_IN], BF16)
        nc.sync.dma_start(out=h_sb[:], in_=h2)
        w1_raw = keep.tile([P, 2, 4, CF], BF16)
        for g in range(2):
            nc.sync.dma_start(
                out=w1_raw[:, g],
                in_=mu_w1_h[512 * g : 512 * (g + 1), :].rearrange("(p j) c -> p j c", j=4),
            )
        sm_raw = keep.tile([P, CF], BF16)
        nc.scalar.dma_start(out=sm_raw[0:NCODE, :], in_=code_mu)
        nc.scalar.dma_start(out=sm_raw[ROW_B1 : ROW_B1 + 8, :], in_=mu_b1.partition_broadcast(8))
        nc.scalar.dma_start(out=sm_raw[ROW_G : ROW_G + 8, :], in_=ln_g.partition_broadcast(8))
        nc.scalar.dma_start(out=sm_raw[ROW_B : ROW_B + 8, :], in_=ln_b.partition_broadcast(8))
        nc.scalar.dma_start(out=sm_raw[ROW_B2 : ROW_B2 + 8, :], in_=mu_b2.partition_broadcast(8))
        nc.vector.memset(sm_raw[64:128, :].bitcast(F32), 0.0)
        w2_raw = keep.tile([P, 4, CF], BF16)
        nc.sync.dma_start(out=w2_raw[:], in_=mu_w2.rearrange("(p t) n -> p t n", t=4))

        ident = keep.tile([P, P], F32)
        make_identity(nc, ident[:])
        ident_bf = keep.tile([P, P], BF16)
        make_identity(nc, ident_bf[:])
        ones = keep.tile([P, P], F32)
        nc.vector.memset(ones[:], 1.0 / CF)
        halves = keep.tile([P, P], F32)
        nc.vector.memset(halves[:], 0.5)
        eps = keep.tile([P, 1], F32)
        nc.vector.memset(eps[:], LN_EPS)
        warm = keep.tile([P, 1], F32)
        nc.scalar.activation(out=warm[:], in_=eps[:], func=ACT.Abs_reciprocal_sqrt)

        def dummy(n):
            if n == 0:
                return
            busy = pso.tile([P, P], F32, tag="o", name="busy")
            for i in range(n):
                nc.tensor.matmul(busy[:], lhsT=ident[:], rhs=ident[:], start=True, stop=True)

        h_w = h_sb[:].bitcast(F32)
        dummy(D0)
        xt = pso.tile([P, 2, 2, P], F32, tag="o")
        for g in range(2):
            for u in range(2):
                nc.tensor.transpose(
                    xt[:, g, u, :], h_w[:, 256 * g + u : 256 * (g + 1) : 2], ident[:]
                )
        hg = keep.tile([P, 2, TOK, 4], BF16, align_bytes=64)
        nc.scalar.copy(out=hg[:].bitcast(F32), in_=xt[:].rearrange("p g u r -> p g r u"))
        smT_ps = pso.tile([P, 6, P], BF16, tag="o")
        for t in range(4):
            nc.tensor.transpose(smT_ps[:, t, :], sm_raw[:, t : CF : 4], ident_bf[:])
        for j in range(2):
            nc.tensor.transpose(
                smT_ps[:, 4 + j, :], sm_raw[:, P * (2 + j) : P * (3 + j)], ident_bf[:]
            )
        rows_ps = []
        for row in (ROW_B, ROW_B2):
            row_ps = psr.tile([P, CF], F32, tag="r", name="row_ps")
            rows_ps.append(row_ps)
            nc.tensor.matmul(
                row_ps[:],
                lhsT=ident_bf[:, row : row + 1].to_broadcast([P, P]),
                rhs=sm_raw[:],
                start=True,
                stop=True,
            )

        w1g = keep.tile([P, 2, CF, 4], BF16, align_bytes=64)
        w1_codes = keep.tile([P, 2, CF], U32, align_bytes=64)
        w1_scales = keep.tile([P, 2, CF], U8, align_bytes=64)
        h_codes = keep.tile([P, 2 * TOK], U32, align_bytes=64)
        h_scales = keep.tile([P, 2 * TOK], U8, align_bytes=64)

        def quantise_w1(g):
            nc.vector.quantize_mx(
                out=w1_codes[:, g, :].bitcast(FP8X4),
                scales=w1_scales[:, g, :],
                in_=w1g[:, g].rearrange("p c t -> p (c t)"),
            )

        regroup_w1(nc.vector.tensor_copy, w1g[:, 0], w1_raw[:, 0], 0, W1_V // 4)
        regroup_w1(nc.scalar.copy, w1g[:, 0], w1_raw[:, 0], W1_V // 4, P)
        regroup_w1(nc.vector.tensor_copy, w1g[:, 1], w1_raw[:, 1], 0, W1_V2 // 4)
        regroup_w1(nc.scalar.copy, w1g[:, 1], w1_raw[:, 1], W1_V2 // 4, P)
        nc.vector.quantize_mx(
            out=h_codes[:].bitcast(FP8X4),
            scales=h_scales[:],
            in_=hg[:].rearrange("p g r t -> p (g r t)"),
        )
        quantise_w1(0)
        quantise_w1(1)
        smT = keep.tile([P, 6, 64], F32)
        nc.scalar.copy(out=smT[:], in_=smT_ps[:, :, 0:64])
        b_bc = keep.tile([P, CF], F32)
        b2_bc = keep.tile([P, CF], F32)
        nc.scalar.copy(
            out=b_bc[:].rearrange("q (u p e) -> q u p e", u=2, e=2),
            in_=rows_ps[0][:].rearrange("q (p u e) -> q u p e", u=2, e=2),
        )
        nc.scalar.copy(out=b2_bc[:], in_=rows_ps[1][:])
        cm1 = keep.tile([P, 4, NCODE], F32)
        nc.vector.tensor_tensor(
            out=cm1[:],
            in0=smT[:, 0:4, 0:NCODE],
            in1=smT[:, 0:4, ROW_B1 : ROW_B1 + 1].to_broadcast([P, 4, NCODE]),
            op=ALU.add,
        )
        cms = keep.tile([P, NCODE], F32)
        nc.vector.tensor_reduce(
            out=cms[:], in_=cm1[:].rearrange("p t c -> p c t"), axis=AX.X, op=ALU.add
        )
        neg_g = keep.tile([P, 4], F32)
        nc.vector.tensor_scalar_mul(out=neg_g[:], in0=smT[:, 0:4, ROW_G], scalar1=-1.0)
        b_col = keep.tile([P, 4], F32)
        nc.vector.tensor_copy(out=b_col[:], in_=smT[:, 0:4, ROW_B])
        w2g = keep.tile([P, CF, 4], BF16, align_bytes=64)

        def regroup_w2(op, i):
            regroup(op, w2g[:, P * i : P * (i + 1)], w2_raw[:, :, P * i : P * (i + 1)])

        regroup_w2(nc.vector.tensor_copy, 0)

        dummy(D1)
        hpT_ps = [pso.tile([P, TOK], F32, tag="o", name="hpT_ps%d" % t) for t in range(4)]
        hp_ps = pso.tile([P, CF], F32, tag="o")
        for g in range(2):
            nc.tensor.matmul_mx(
                out=hp_ps[:],
                lhsT=h_codes[:, TOK * g : TOK * (g + 1)].bitcast(FP8X4),
                lhsT_scale=h_scales[:, TOK * g : TOK * (g + 1)],
                rhs=w1_codes[:, g, :].bitcast(FP8X4),
                rhs_scale=w1_scales[:, g, :],
                start=(g == 0),
                stop=(g == 1),
            )
            for t in range(4):
                nc.tensor.matmul_mx(
                    out=hpT_ps[t][:],
                    lhsT=w1_codes[:, g, P * t : P * (t + 1)].bitcast(FP8X4),
                    lhsT_scale=w1_scales[:, g, P * t : P * (t + 1)],
                    rhs=h_codes[:, TOK * g : TOK * (g + 1)].bitcast(FP8X4),
                    rhs_scale=h_scales[:, TOK * g : TOK * (g + 1)],
                    start=(g == 0),
                    stop=(g == 1),
                )
            if g == 0:
                mc_ps = psr.tile([P, NCODE], F32, tag="r")
        nc.tensor.matmul(mc_ps[:], lhsT=ones[:], rhs=cms[:], start=True, stop=True)
        dummy(D3)
        c_sb = keep.tile([P, 4, NCODE], F32)
        st = keep.tile([P, 6], F32)
        nc.vector.bn_stats(out=st[:], in_=hp_ps[:])
        mv = keep.tile([P, 2], F32)
        nc.vector.bn_aggr(out=mv[:], in_=st[:])
        nc.vector.tensor_tensor(
            out=c_sb[:],
            in0=cm1[:],
            in1=mc_ps[:].unsqueeze(1).to_broadcast([P, 4, NCODE]),
            op=ALU.subtract,
        )
        hpT = keep.tile([P, 4, TOK], F32)
        for t in range(4):
            nc.scalar.copy(out=hpT[:, t, :], in_=hpT_ps[t][:])
        hpTg = keep.tile([P, 4, TOK], F32)
        for t in range(4):
            nc.scalar.activation(
                out=hpTg[:, t, :], in_=hpT_ps[t][:], func=ACT.Copy, scale=smT[:, t, ROW_G : ROW_G + 1]
            )
        regroup_w2(nc.scalar.copy, 1)
        csq = keep.tile([P, 4, NCODE], F32)
        nc.vector.tensor_tensor(out=csq[:], in0=c_sb[:], in1=c_sb[:], op=ALU.mult)
        cvs = keep.tile([P, NCODE], F32)
        nc.vector.tensor_reduce(
            out=cvs[:], in_=csq[:].rearrange("p t c -> p c t"), axis=AX.X, op=ALU.add
        )
        vhe = keep.tile([P, 1], F32)
        nc.vector.tensor_scalar_add(out=vhe[:], in0=mv[:, 1:2], scalar1=LN_EPS)
        cg = keep.tile([P, 4, NCODE], F32)
        nc.vector.tensor_tensor(
            out=cg[:],
            in0=c_sb[:],
            in1=smT[:, 0:4, ROW_G : ROW_G + 1].to_broadcast([P, 4, NCODE]),
            op=ALU.mult,
        )

        mh_ps = pso.tile([P, TOK], F32, tag="o")
        nc.tensor.transpose(mh_ps[:], mv[:, 0:1].to_broadcast([P, P]), ident[:])
        v_ps = pso.tile([P, NCODE], F32, tag="o")
        for t in range(4):
            nc.tensor.matmul(v_ps[:], lhsT=hpT[:, t, :], rhs=c_sb[:, t, :], start=(t == 0), stop=False)
        nc.tensor.matmul(v_ps[:], lhsT=halves[:], rhs=cvs[:], start=False, stop=True)
        dummy(D2)
        r_sb = keep.tile([P, NCODE], F32)
        nc.scalar.activation(
            out=r_sb[:], in_=v_ps[:], func=ACT.Abs_reciprocal_sqrt, bias=vhe[:, 0:1], scale=2.0 / CF
        )
        nc.scalar.activation(out=warm[:], in_=eps[:], func=ACT.Tanh)
        w2_codes = keep.tile([P, CF], U32, align_bytes=64)
        w2_scales = keep.tile([P, CF], U8, align_bytes=64)
        a_sb = keep.tile([P, 4, TOK], F32)
        for t in range(4):
            nc.vector.scalar_tensor_tensor(
                out=a_sb[:, t, :],
                in0=mh_ps[:],
                scalar=neg_g[:, t : t + 1],
                in1=hpTg[:, t, :],
                op0=ALU.mult,
                op1=ALU.add,
            )

        regroup_w2(nc.vector.tensor_copy, 2)
        regroup_w2(nc.vector.tensor_copy, 3)

        def quantise_w2():
            nc.vector.quantize_mx(
                out=w2_codes[:].bitcast(FP8X4),
                scales=w2_scales[:],
                in_=w2g[:].rearrange("p c t -> p (c t)"),
            )

        tiles = {}

        def codes_of(rd, kinds):
            return [cl for cl in range(len(KINDS[rd])) if KINDS[rd][cl] in kinds]

        def bcast_r(rd):
            cls = codes_of(rd, "gvS")
            if not cls:
                return
            r_ps = psr.tile([P, 4, TOK], F32, tag="r", name="r_ps")
            tiles[("rt", rd)] = r_ps
            for i, cl in enumerate(cls):
                code = FIRST[rd] + cl
                tiles[("r", rd, cl)] = r_ps[:, i, :]
                nc.tensor.transpose(
                    r_ps[:, i, :], r_sb[:, code : code + 1].to_broadcast([P, P]), ident[:]
                )

        def normalise(rd, cls):
            if ("z", rd) not in tiles:
                z = work.tile([P, 4, 4, TOK], F32, name="z")
                tiles[("z", rd)] = z
            z = tiles[("z", rd)]
            for cl in cls:
                code = FIRST[rd] + cl
                for t in range(4):
                    nc.vector.scalar_tensor_tensor(
                        out=z[:, t, cl, :],
                        in0=a_sb[:, t, :],
                        scalar=cg[:, t, code : code + 1],
                        in1=tiles[("r", rd, cl)],
                        op0=ALU.add,
                        op1=ALU.mult,
                    )

        def token():
            nc.vector.tensor_copy(out=b_col[:], in_=smT[:, 0:4, ROW_B])

        def mg_of(rd):
            if ("mg", rd) not in tiles:
                mg = work.tile([P, len(KINDS[rd]) * TOK, 4], BF16, align_bytes=64, name="mg")
                tiles[("mg", rd)] = mg
            return tiles[("mg", rd)]

        def add_bias(rd, kind, cls=None):
            engine = nc.gpsimd if kind == "g" else nc.vector
            for cl in codes_of(rd, kind) if cls is None else cls:
                engine.tensor_tensor(
                    out=mg_of(rd)[:, TOK * cl : TOK * (cl + 1), :],
                    in0=tiles[("z", rd)][:, :, cl, :].rearrange("p t r -> p r t"),
                    in1=b_col[:].unsqueeze(1).to_broadcast([P, TOK, 4]),
                    op=ALU.add,
                )

        def bias_planes(rd):
            cls = codes_of(rd, "S")
            if not cls:
                return
            m = work.tile([P, 4, len(cls), TOK], BF16, name="m")
            for t in range(4):
                nc.scalar.activation(
                    out=m[:, t],
                    in_=tiles[("z", rd)][:, t, cls[0] : cls[-1] + 1, :],
                    func=ACT.Identity,
                    bias=b_col[:, t : t + 1],
                )
            regroup(
                nc.scalar.copy,
                mg_of(rd)[:, TOK * cls[0] : TOK * (cls[-1] + 1), :],
                m[:].rearrange("p t c r -> p t (c r)"),
            )

        def sum_rows(rd):
            for cl in codes_of(rd, "e"):
                code = FIRST[rd] + cl
                u = pso.tile([P, 4, P], F32, tag="o", name="u")
                tiles[("u", rd, cl)] = u
                for t in range(4):
                    nc.tensor.matmul(
                        u[:, t, :], lhsT=a_sb[:, t, :], rhs=ident[:], start=True, stop=False, is_transpose=True
                    )
                    nc.tensor.matmul(
                        u[:, t, :],
                        lhsT=cg[:, t, code : code + 1].to_broadcast([P, P]),
                        rhs=ident[:],
                        start=False,
                        stop=True,
                        is_transpose=True,
                    )

        def scale_rows(rd):
            for cl in codes_of(rd, "e"):
                code = FIRST[rd] + cl
                x = work.tile([P, CF], BF16, name="x")
                tiles[("x", rd, cl)] = x
                for u in range(2):
                    half = slice(2 * P * u, 2 * P * (u + 1))
                    nc.vector.scalar_tensor_tensor(
                        out=x[:, half].rearrange("p (r e) -> p r e", e=2),
                        in0=tiles[("u", rd, cl)][:, 2 * u : 2 * u + 2, :].rearrange("p e r -> p r e"),
                        scalar=r_sb[:, code : code + 1],
                        in1=b_bc[:, half].rearrange("p (r e) -> p r e", e=2),
                        op0=ALU.mult,
                        op1=ALU.add,
                    )

        def turn_rows(rd):
            cls = codes_of(rd, "e")
            if not cls:
                return
            xt_ps = pso.tile([P, len(cls), 2, TOK], F32, tag="o", name="xt_ps")
            tiles[("xt", rd)] = xt_ps
            for i, cl in enumerate(cls):
                words = tiles[("x", rd, cl)][:].bitcast(F32)
                for u in range(2):
                    nc.tensor.transpose(xt_ps[:, i, u, :], words[:, P * u : P * (u + 1)], ident[:])

        def copy_rows(rd):
            cls = codes_of(rd, "e")
            if not cls:
                return
            part = mg_of(rd)[:, TOK * cls[0] : TOK * (cls[-1] + 1), :].bitcast(F32)
            nc.scalar.copy(
                out=part.rearrange("p (c r) u -> p c r u", r=TOK),
                in_=tiles[("xt", rd)][:].rearrange("p c u r -> p c r u"),
            )

        def quantise_mu(rd):
            w = len(KINDS[rd]) * TOK
            mu_codes = work.tile([P, w], U32, align_bytes=64, name="mu_codes")
            mu_scales = work.tile([P, w], U8, align_bytes=64, name="mu_scales")
            tiles[("q", rd)] = (mu_codes, mu_scales)
            nc.vector.quantize_mx(
                out=mu_codes[:].bitcast(FP8X4),
                scales=mu_scales[:],
                in_=mg_of(rd)[:].rearrange("p w t -> p (w t)"),
            )

        def wide(rd):
            return CF - P * KB[rd]

        def a_groups(rd):
            return range(0, len(KINDS[rd]), CF // wide(rd))

        def blocks(rd):
            return range(BLK - KB[rd], BLK)

        def mm_a(rd):
            mu_codes, mu_scales = tiles[("q", rd)]
            wa = wide(rd)
            per = CF // wa
            res = work.tile([P, len(KINDS[rd]), CF], F32, name="res")
            tiles[("res", rd)] = res
            for c0 in a_groups(rd):
                o_ps = pso.tile([P, per, wa], F32, tag="o", name="oa_ps")
                tiles[("oa", rd, c0)] = o_ps
                for i in range(per):
                    cl = c0 + i
                    nc.tensor.matmul_mx(
                        out=o_ps[:, i, :],
                        lhsT=mu_codes[:, TOK * cl : TOK * (cl + 1)].bitcast(FP8X4),
                        lhsT_scale=mu_scales[:, TOK * cl : TOK * (cl + 1)],
                        rhs=w2_codes[:, 0:wa].bitcast(FP8X4),
                        rhs_scale=w2_scales[:, 0:wa],
                        start=True,
                        stop=True,
                    )

        def mm_b(rd):
            mu_codes, mu_scales = tiles[("q", rd)]
            for nb in blocks(rd):
                o_ps = pso.tile([P, len(KINDS[rd]) * TOK], F32, tag="o", name="ob_ps")
                tiles[("ob", rd, nb)] = o_ps
                nc.tensor.matmul_mx(
                    out=o_ps[:],
                    lhsT=w2_codes[:, P * nb : P * (nb + 1)].bitcast(FP8X4),
                    lhsT_scale=w2_scales[:, P * nb : P * (nb + 1)],
                    rhs=mu_codes[:].bitcast(FP8X4),
                    rhs_scale=mu_scales[:],
                    start=True,
                    stop=True,
                )

        def tanh_b(rd):
            for nb in blocks(rd):
                th = work.tile([P, len(KINDS[rd]) * TOK], F32, name="th")
                tiles[("th", rd, nb)] = th
                nc.scalar.activation(
                    out=th[:],
                    in_=tiles[("ob", rd, nb)][:],
                    func=ACT.Tanh,
                    bias=smT[:, 2 + nb, ROW_B2 : ROW_B2 + 1],
                )

        def turn_b(rd):
            for nb in blocks(rd):
                tr = pso.tile([P, len(KINDS[rd]), P], F32, tag="o", name="tr")
                tiles[("tr", rd, nb)] = tr
                for cl in range(len(KINDS[rd])):
                    nc.tensor.transpose(
                        tr[:, cl, :], tiles[("th", rd, nb)][:, TOK * cl : TOK * (cl + 1)], ident[:]
                    )

        def copy_b(rd):
            for nb in blocks(rd):
                nc.scalar.copy(
                    out=tiles[("res", rd)][:, :, P * nb : P * (nb + 1)], in_=tiles[("tr", rd, nb)][:]
                )

        def add_a(rd, c0, lo=0, hi=CF):
            wa = wide(rd)
            hi = min(hi, wa)
            per = CF // wa
            nc.vector.tensor_tensor(
                out=tiles[("res", rd)][:, c0 : c0 + per, lo:hi],
                in0=tiles[("oa", rd, c0)][:, :, lo:hi],
                in1=b2_bc[:, lo:hi].unsqueeze(1).to_broadcast([P, per, hi - lo]),
                op=ALU.add,
            )

        def tanh_a(rd, c0, lo=0, hi=CF):
            hi = min(hi, wide(rd))
            part = tiles[("res", rd)][:, c0 : c0 + CF // wide(rd), lo:hi]
            nc.scalar.activation(out=part, in_=part, func=ACT.Tanh)

        def store(rd, c0, c1, lo=0, hi=CF):
            nc.sync.dma_start(
                out=out3[:, FIRST[rd] + c0 : FIRST[rd] + c1, lo:hi],
                in_=tiles[("res", rd)][:, c0:c1, lo:hi],
            )

        last = ROUNDS - 1
        bcast_r(0)
        bcast_r(1)
        sum_rows(1)
        dummy(DA)
        normalise(0, codes_of(0, "gvS"))
        add_bias(0, "g")
        add_bias(0, "v")
        bias_planes(0)
        scale_rows(1)
        turn_rows(1)
        quantise_w2()
        normalise(1, codes_of(1, "gvS")[:HALF1])
        for rd in range(last):
            quantise_mu(rd)
            token()
            mm_a(rd)
            mm_b(rd)
            if rd == 0:
                bcast_r(2)
                sum_rows(2)
                dummy(DB)
                normalise(1, codes_of(1, "gvS")[HALF1:])
            else:
                if rd + 2 < ROUNDS:
                    sum_rows(rd + 2)
                    dummy(DC)
            if rd < last - 1 or not G8:
                add_bias(rd + 1, "g")
            else:
                add_bias(last, "g", codes_of(last, "g")[1:])
            if rd == last - 2 and G8:
                late_g = True
            else:
                late_g = False
            if rd > 0:
                copy_b(rd - 1)
                if KB[rd - 1]:
                    store(rd - 1, 0, len(KINDS[rd - 1]), wide(rd - 1) if rd - 1 >= SPLIT else 0)
            copy_rows(rd + 1)
            tanh_b(rd)
            turn_b(rd)
            if rd == 0:
                for c0 in a_groups(rd):
                    add_a(rd, c0)
            if rd + 2 < ROUNDS:
                normalise(rd + 2, codes_of(rd + 2, "gvS"))
            if late_g:
                add_bias(last, "g", codes_of(last, "g")[:1])
            groups = list(a_groups(rd))
            ahead = 0
            if rd == last - 1:
                ahead = TAIL
                bias_planes(last)
                add_bias(last, "v")
                for c0 in groups[:ahead]:
                    add_a(rd, c0)
                quantise_mu(last)
                mm_a(last)
            if rd > 0:
                for c0 in groups[ahead:]:
                    add_a(rd, c0)
            for c0 in a_groups(rd):
                tanh_a(rd, c0)
                if KB[rd] == 0:
                    store(rd, c0, c0 + 1)
                elif rd >= SPLIT:
                    store(rd, c0, c0 + CF // wide(rd), 0, wide(rd))
            if rd < last - 1:
                add_bias(rd + 1, "v")
            if rd + 3 < ROUNDS:
                bcast_r(rd + 3)
            if rd + 2 < ROUNDS:
                scale_rows(rd + 2)
                turn_rows(rd + 2)
        copy_b(last - 1)
        if KB[last - 1]:
            store(last - 1, 0, len(KINDS[last - 1]))
        n = len(KINDS[last])
        for c0 in range(n - 1):
            add_a(last, c0)
            tanh_a(last, c0)
            store(last, c0, c0 + 1)
        for lo in (0, CF // 2):
            add_a(last, n - 1, lo, lo + CF // 2)
            tanh_a(last, n - 1, lo, lo + CF // 2)
            store(last, n - 1, n, lo, lo + CF // 2)
